import numpy as np
import ml_dtypes


def mxq(x, axis, fmt="e4m3"):
    dtype, down = {"e4m3": (ml_dtypes.float8_e4m3fn, 7), "e5m2": (ml_dtypes.float8_e5m2, 14)}[fmt]
    v = np.moveaxis(np.asarray(x, np.float32).astype(ml_dtypes.bfloat16).astype(np.float64), axis, -1)
    blocks = v.reshape(v.shape[:-1] + (-1, 32))
    amax = np.abs(blocks).max(-1, keepdims=True)
    byte = np.maximum(np.where(amax > 0, np.frexp(amax)[1] - 1 + 127, 0) - down, 1)
    scale = np.exp2(byte - 127.0)
    codes = (blocks / scale).astype(np.float32).astype(dtype).astype(np.float64)
    return np.moveaxis((codes * scale).reshape(v.shape), -1, axis)


WIDE = False


def mx_kscale(k):
    if not WIDE:
        return np.ones(k)
    levels = np.array([10, -10, 5, -5, 0])
    a = np.random.permutation(np.resize(levels, k // 512 * 4)).reshape(k // 512, 4)
    idx = np.arange(k)
    return np.exp2(a[idx // 512, idx % 128 // 32])


BF16 = ml_dtypes.bfloat16


def bf(x):
    return np.asarray(x, np.float32).astype(BF16)


def f64(x):
    return np.asarray(x).astype(np.float64)


B, D_IN, D_H = 4096, 512, 512


def sigmoid(v):
    return 1.0 / (1.0 + np.exp(-v))


def setup_inputs():
    s, t = mx_kscale(D_IN), mx_kscale(D_H)

    def w_in():
        return bf(np.random.standard_normal((D_H, D_IN)) * 0.6 / np.sqrt(D_IN) / s[None, :])

    def w_rec():
        return bf(np.random.standard_normal((D_H, D_H)) * 0.6 / np.sqrt(D_H) / t[None, :])

    def bias():
        return bf(np.random.standard_normal(D_H) * 0.3)

    return {"incoming": bf(np.random.standard_normal((B, D_IN)) * s), "h": bf(np.random.standard_normal((B, D_H)) * t),
            "c": bf(np.random.standard_normal((B, D_H))), "gated_cand": bf(np.random.standard_normal((B, D_H)) * 0.5),
            "W_f": w_in(), "b_W_f": bias(), "W_o": w_in(), "b_W_o": bias(),
            "U_f": w_rec(), "b_U_f": bias(), "U_o": w_rec(), "b_U_o": bias()}


def reference(incoming, h, c, gated_cand, W_f, b_W_f, W_o, b_W_o, U_f, b_U_f, U_o, b_U_o):
    xq = mxq(f64(incoming), 1, "e4m3")
    hq = mxq(f64(h), 1, "e4m3")
    O = sigmoid((xq @ mxq(f64(W_o), 1, "e4m3").T) + f64(b_W_o) + (hq @ mxq(f64(U_o), 1, "e4m3").T) + f64(b_U_o))
    F = sigmoid((xq @ mxq(f64(W_f), 1, "e4m3").T) + f64(b_W_f) + (hq @ mxq(f64(U_f), 1, "e4m3").T) + f64(b_U_f))
    C = F * f64(c) + f64(gated_cand)
    H = O * np.tanh(C)
    return (H, C)

@@ -1,0 +1,227 @@
+from contextlib import ExitStack
+
+import concourse.mybir as mybir
+from concourse.masks import make_identity
+
+F32 = mybir.dt.float32
+BF16 = mybir.dt.bfloat16
+U32 = mybir.dt.uint32
+U8 = mybir.dt.uint8
+FP8X4 = mybir.dt.float8_e4m3fn_x4
+ACT = mybir.ActivationFunctionType
+ALU = mybir.AluOpType
+
+P = 128
+PACK = 4
+BATCH = 4096
+D = 512
+BANK = 512
+PSUM_BANKS = 8
+ROW_TILES = BATCH // P
+TILES = 4
+CHUNK_ROWS = TILES * P
+CHUNKS = ROW_TILES // TILES
+FEATURE_TILES = D // P
+STORE_TILES = 2
+LOADS_AHEAD = 3
+
+FLOPS = 4 * 2 * BATCH * D * D
+
+
+def tile_lstmcell_pb_t_kernel(
+    tc, incoming, h, c, gated_cand, W_f, b_W_f, W_o, b_W_o, U_f, b_U_f, U_o, b_U_o, out_0, out_1
+):
+    nc = tc.nc
+
+    def by_row_tile(ap):
+        return ap.rearrange("(p t) d -> p t d", t=ROW_TILES)
+
+    def by_feature_tile(ap):
+        return ap.rearrange("(a p) k -> p a k", p=P)
+
+    with ExitStack() as ctx:
+        const = ctx.enter_context(tc.tile_pool(name="const", bufs=1))
+        acts = ctx.enter_context(tc.tile_pool(name="acts", bufs=LOADS_AHEAD))
+        state = ctx.enter_context(tc.tile_pool(name="state", bufs=LOADS_AHEAD + 1))
+        stage = ctx.enter_context(tc.tile_pool(name="stage", bufs=3))
+        mxops = ctx.enter_context(tc.tile_pool(name="mxops", bufs=2))
+        gates = ctx.enter_context(tc.tile_pool(name="gates", bufs=2))
+        outs = ctx.enter_context(tc.tile_pool(name="outs", bufs=3))
+        banks = ctx.enter_context(tc.psum_pool(name="banks", bufs=PSUM_BANKS))
+        ctx.enter_context(tc.manual_schedule())
+
+        def load(view, first_tile, pool, tag):
+            rows = pool.tile([P, TILES * D], BF16, name=tag, tag=tag)
+            nc.sync.dma_start(
+                out=rows[:].rearrange("p (t d) -> p t d", t=TILES),
+                in_=view[:, first_tile : first_tile + TILES, :],
+            )
+            return rows
+
+        def k_to_partitions(rows, scalar_helps):
+            grouped = stage.tile([P, TILES * P * PACK], BF16, name="grouped", tag="grouped", align_bytes=64)
+            row_words = rows[:].bitcast(F32).rearrange("r (t u q) -> r t u q", t=TILES, u=2)
+            grouped_words = grouped[:].bitcast(F32).rearrange("q (t r u) -> q t r u", t=TILES, u=2)
+            for pair in range(TILES // 2):
+                bank = banks.tile([P, BANK], F32, name="bank", tag="bank")
+                turned = bank[:].rearrange("q (i u r) -> q i u r", i=2, u=2)
+                for i in range(2):
+                    for u in range(2):
+                        nc.tensor.transpose(turned[:, i, u, :], row_words[:, 2 * pair + i, u, :], ident[:])
+                side_by_side = turned.rearrange("q i u r -> q i r u")
+                if scalar_helps and pair == 1:
+                    nc.scalar.copy(out=grouped_words[:, 2 * pair : 2 * pair + 2, :, :], in_=side_by_side)
+                else:
+                    nc.vector.tensor_copy(out=grouped_words[:, 2 * pair : 2 * pair + 2, :, :], in_=side_by_side)
+            return grouped
+
+        def quantise(grouped, pool, tag):
+            codes = pool.tile([P, TILES * P], U32, name="codes_" + tag, tag="codes_" + tag, align_bytes=64)
+            scales = pool.tile([P, TILES * P], U8, name="scales_" + tag, tag="scales_" + tag, align_bytes=64)
+            nc.vector.quantize_mx(out=codes[:].bitcast(FP8X4), scales=scales[:], in_=grouped[:])
+            return codes, scales
+
+        def gate_by_feature(w_in, w_rec, x_q, h_q, first_bias, tag):
+            gate = gates.tile([P, FEATURE_TILES * CHUNK_ROWS], F32, name=tag, tag=tag)
+            for a in range(FEATURE_TILES):
+                features = slice(a * P, (a + 1) * P)
+                acc = banks.tile([P, BANK], F32, name="bank", tag="bank")
+                for step, (weight, moving) in enumerate(((w_in, x_q), (w_rec, h_q))):
+                    nc.tensor.matmul_mx(
+                        out=acc[:],
+                        lhsT=weight[0][:, features].bitcast(FP8X4),
+                        lhsT_scale=weight[1][:, features],
+                        rhs=moving[0][:].bitcast(FP8X4),
+                        rhs_scale=moving[1][:],
+                        start=(step == 0),
+                        stop=(step == 1),
+                    )
+                nc.scalar.activation(
+                    out=gate[:, a * CHUNK_ROWS : (a + 1) * CHUNK_ROWS],
+                    in_=acc[:],
+                    func=ACT.Sigmoid,
+                    bias=gate_bias[:, first_bias + a : first_bias + a + 1],
+                    scale=1.0,
+                )
+            return gate
+
+        def gate_by_row(gate, t):
+            bank = banks.tile([P, BANK], F32, name="bank", tag="bank")
+            for a in range(FEATURE_TILES):
+                first = a * CHUNK_ROWS + t * P
+                nc.tensor.transpose(bank[:, a * P : (a + 1) * P], gate[:, first : first + P], ident[:])
+            return bank
+
+        def store(view, j, t, result):
+            if (t + 1) % STORE_TILES == 0:
+                first = t + 1 - STORE_TILES
+                nc.sync.dma_start(
+                    out=view[:, j * TILES + first : j * TILES + t + 1, :],
+                    in_=result[:, first * D : (t + 1) * D].rearrange("p (t d) -> p t d", t=STORE_TILES),
+                )
+
+        ident = const.tile([P, P], F32, name="ident")
+        make_identity(nc, ident[:])
+
+        zero = const.tile([P, 1], F32, name="zero")
+        nc.vector.memset(zero[:], 0.0)
+        unused = const.tile([P, 1], F32, name="unused")
+        nc.scalar.activation(out=unused[:], in_=zero[:], func=ACT.Sigmoid)
+
+        x_view, h_view = by_row_tile(incoming), by_row_tile(h)
+        c_view, cand_view = by_row_tile(c), by_row_tile(gated_cand)
+        h_out, c_out = by_row_tile(out_0), by_row_tile(out_1)
+        x_rows, h_rows, c_rows, cand_rows = {}, {}, {}, {}
+
+        def load_acts(j):
+            x_rows[j] = load(x_view, j * TILES, acts, "x")
+            h_rows[j] = load(h_view, j * TILES, acts, "h")
+
+        def load_state(j):
+            c_rows[j] = load(c_view, j * TILES, state, "c")
+            cand_rows[j] = load(cand_view, j * TILES, state, "cand")
+
+        w_f_rows = load(by_feature_tile(W_f), 0, const, "W_f")
+        u_f_rows = load(by_feature_tile(U_f), 0, const, "U_f")
+        load_acts(0)
+        w_o_rows = load(by_feature_tile(W_o), 0, const, "W_o")
+        u_o_rows = load(by_feature_tile(U_o), 0, const, "U_o")
+        load_acts(1)
+        load_state(0)
+        load_acts(2)
+        load_state(1)
+        load_state(2)
+
+        bias_rows = const.tile([P, P], BF16, name="bias_rows")
+        nc.gpsimd.memset(bias_rows[:], 0.0)
+        for v, vector in enumerate((b_W_f, b_W_o, b_U_f, b_U_o)):
+            nc.scalar.dma_start(
+                out=bias_rows[v * FEATURE_TILES : (v + 1) * FEATURE_TILES, :],
+                in_=vector.rearrange("(a p) -> a p", p=P),
+            )
+
+        x_q, h_q = {}, {}
+        w_f_q = quantise(k_to_partitions(w_f_rows, True), const, "W_f")
+        u_f_q = quantise(k_to_partitions(u_f_rows, True), const, "U_f")
+        x_q[0] = quantise(k_to_partitions(x_rows[0], True), mxops, "x")
+        h_q[0] = quantise(k_to_partitions(h_rows[0], True), mxops, "h")
+
+        bias_rows_f32 = const.tile([P, P], F32, name="bias_rows_f32")
+        nc.vector.tensor_copy(out=bias_rows_f32[:], in_=bias_rows[:])
+        bias_bank = banks.tile([P, BANK], F32, name="bank", tag="bank")
+        nc.tensor.transpose(bias_bank[:, 0:P], bias_rows_f32[:], ident[:])
+        bias_columns = const.tile([P, 4 * FEATURE_TILES], F32, name="bias_columns")
+        nc.vector.tensor_copy(out=bias_columns[:], in_=bias_bank[:, 0 : 4 * FEATURE_TILES])
+        gate_bias = const.tile([P, 2 * FEATURE_TILES], F32, name="gate_bias")
+        nc.vector.tensor_tensor(
+            out=gate_bias[:],
+            in0=bias_columns[:, 0 : 2 * FEATURE_TILES],
+            in1=bias_columns[:, 2 * FEATURE_TILES : 4 * FEATURE_TILES],
+            op=ALU.add,
+        )
+        FORGET_BIAS, OUTPUT_BIAS = 0, FEATURE_TILES
+
+        for j in range(CHUNKS):
+            if j + LOADS_AHEAD < CHUNKS:
+                load_acts(j + LOADS_AHEAD)
+                load_state(j + LOADS_AHEAD)
+
+            forget = gate_by_feature(w_f_q, u_f_q, x_q[j], h_q[j], FORGET_BIAS, "forget")
+
+            if j == 0:
+                w_o_q = quantise(k_to_partitions(w_o_rows, True), const, "W_o")
+                u_o_q = quantise(k_to_partitions(u_o_rows, True), const, "U_o")
+                x_q[1] = quantise(k_to_partitions(x_rows[1], True), mxops, "x")
+            if j + 1 < CHUNKS:
+                h_grouped = k_to_partitions(h_rows[j + 1], True)
+
+            c_new = outs.tile([P, TILES * D], F32, name="c_new", tag="c_new")
+            for t in range(TILES):
+                cols = slice(t * D, (t + 1) * D)
+                forget_rows = gate_by_row(forget, t)
+                nc.vector.tensor_tensor(out=c_new[:, cols], in0=forget_rows[:], in1=c_rows[j][:, cols], op=ALU.mult)
+                nc.gpsimd.tensor_tensor(out=c_new[:, cols], in0=c_new[:, cols], in1=cand_rows[j][:, cols], op=ALU.add)
+                store(c_out, j, t, c_new)
+
+            if j + 1 < CHUNKS:
+                h_q[j + 1] = quantise(h_grouped, mxops, "h")
+
+            output = gate_by_feature(w_o_q, u_o_q, x_q[j], h_q[j], OUTPUT_BIAS, "output")
+
+            tanh_c = outs.tile([P, TILES * D], F32, name="tanh_c", tag="tanh_c")
+            for t in range(TILES):
+                cols = slice(t * D, (t + 1) * D)
+                nc.scalar.activation(out=tanh_c[:, cols], in_=c_new[:, cols], func=ACT.Tanh)
+
+            if j + 2 < CHUNKS:
+                x_grouped = k_to_partitions(x_rows[j + 2], False)
+
+            h_new = outs.tile([P, TILES * D], F32, name="h_new", tag="h_new")
+            for t in range(TILES):
+                cols = slice(t * D, (t + 1) * D)
+                output_rows = gate_by_row(output, t)
+                nc.vector.tensor_tensor(out=h_new[:, cols], in0=output_rows[:], in1=tanh_c[:, cols], op=ALU.mult)
+                store(h_out, j, t, h_new)
+
+            if j + 2 < CHUNKS:
+                x_q[j + 2] = quantise(x_grouped, mxops, "x")

@@ -200,7 +200,7 @@ def tile_lstmcell_pb_t_kernel(
                 cols = slice(t * D, (t + 1) * D)
                 forget_rows = gate_by_row(forget, t)
                 nc.vector.tensor_tensor(out=c_new[:, cols], in0=forget_rows[:], in1=c_rows[j][:, cols], op=ALU.mult)
-                nc.gpsimd.tensor_tensor(out=c_new[:, cols], in0=c_new[:, cols], in1=cand_rows[j][:, cols], op=ALU.add)
+                nc.vector.tensor_tensor(out=c_new[:, cols], in0=c_new[:, cols], in1=cand_rows[j][:, cols], op=ALU.add)
                 store(c_out, j, t, c_new)
 
             if j + 1 < CHUNKS:

@@ -43,7 +43,7 @@ def tile_lstmcell_pb_t_kernel(
         const = ctx.enter_context(tc.tile_pool(name="const", bufs=1))
         acts = ctx.enter_context(tc.tile_pool(name="acts", bufs=LOADS_AHEAD))
         state = ctx.enter_context(tc.tile_pool(name="state", bufs=LOADS_AHEAD + 1))
-        stage = ctx.enter_context(tc.tile_pool(name="stage", bufs=3))
+        stage = ctx.enter_context(tc.tile_pool(name="stage", bufs=2))
         mxops = ctx.enter_context(tc.tile_pool(name="mxops", bufs=2))
         gates = ctx.enter_context(tc.tile_pool(name="gates", bufs=2))
         outs = ctx.enter_context(tc.tile_pool(name="outs", bufs=3))
@@ -58,22 +58,22 @@ def tile_lstmcell_pb_t_kernel(
             )
             return rows
 
-        def k_to_partitions(rows, scalar_helps):
-            grouped = stage.tile([P, TILES * P * PACK], BF16, name="grouped", tag="grouped", align_bytes=64)
+        def new_grouped(tag):
+            return stage.tile([P, TILES * P * PACK], BF16, name="grouped_" + tag, tag="grouped_" + tag, align_bytes=64)
+
+        def k_to_partitions(rows, grouped, pair, on_scalar):
             row_words = rows[:].bitcast(F32).rearrange("r (t u q) -> r t u q", t=TILES, u=2)
             grouped_words = grouped[:].bitcast(F32).rearrange("q (t r u) -> q t r u", t=TILES, u=2)
-            for pair in range(TILES // 2):
-                bank = banks.tile([P, BANK], F32, name="bank", tag="bank")
-                turned = bank[:].rearrange("q (i u r) -> q i u r", i=2, u=2)
-                for i in range(2):
-                    for u in range(2):
-                        nc.tensor.transpose(turned[:, i, u, :], row_words[:, 2 * pair + i, u, :], ident[:])
-                side_by_side = turned.rearrange("q i u r -> q i r u")
-                if scalar_helps and pair == 1:
-                    nc.scalar.copy(out=grouped_words[:, 2 * pair : 2 * pair + 2, :, :], in_=side_by_side)
-                else:
-                    nc.vector.tensor_copy(out=grouped_words[:, 2 * pair : 2 * pair + 2, :, :], in_=side_by_side)
-            return grouped
+            bank = banks.tile([P, BANK], F32, name="bank", tag="bank")
+            turned = bank[:].rearrange("q (i u r) -> q i u r", i=2, u=2)
+            for i in range(2):
+                for u in range(2):
+                    nc.tensor.transpose(turned[:, i, u, :], row_words[:, 2 * pair + i, u, :], ident[:])
+            side_by_side = turned.rearrange("q i u r -> q i r u")
+            if on_scalar:
+                nc.scalar.copy(out=grouped_words[:, 2 * pair : 2 * pair + 2, :, :], in_=side_by_side)
+            else:
+                nc.vector.tensor_copy(out=grouped_words[:, 2 * pair : 2 * pair + 2, :, :], in_=side_by_side)
 
         def quantise(grouped, pool, tag):
             codes = pool.tile([P, TILES * P], U32, name="codes_" + tag, tag="codes_" + tag, align_bytes=64)
@@ -81,12 +81,17 @@ def tile_lstmcell_pb_t_kernel(
             nc.vector.quantize_mx(out=codes[:].bitcast(FP8X4), scales=scales[:], in_=grouped[:])
             return codes, scales
 
-        def gate_by_feature(w_in, w_rec, x_q, h_q, first_bias, tag):
-            gate = gates.tile([P, FEATURE_TILES * CHUNK_ROWS], F32, name=tag, tag=tag)
-            for a in range(FEATURE_TILES):
+        def prepare(rows, pool, tag):
+            grouped = new_grouped("first")
+            k_to_partitions(rows, grouped, 0, False)
+            k_to_partitions(rows, grouped, 1, True)
+            return quantise(grouped, pool, tag)
+
+        def half_gate(gate, half, w_in, w_rec, j, first_bias):
+            for a in range(2 * half, 2 * half + 2):
                 features = slice(a * P, (a + 1) * P)
                 acc = banks.tile([P, BANK], F32, name="bank", tag="bank")
-                for step, (weight, moving) in enumerate(((w_in, x_q), (w_rec, h_q))):
+                for step, (weight, moving) in enumerate(((w_in, x_q[j]), (w_rec, h_q[j]))):
                     nc.tensor.matmul_mx(
                         out=acc[:],
                         lhsT=weight[0][:, features].bitcast(FP8X4),
@@ -103,7 +108,6 @@ def tile_lstmcell_pb_t_kernel(
                     bias=gate_bias[:, first_bias + a : first_bias + a + 1],
                     scale=1.0,
                 )
-            return gate
 
         def gate_by_row(gate, t):
             bank = banks.tile([P, BANK], F32, name="bank", tag="bank")
@@ -119,6 +123,23 @@ def tile_lstmcell_pb_t_kernel(
                     out=view[:, j * TILES + first : j * TILES + t + 1, :],
                     in_=result[:, first * D : (t + 1) * D].rearrange("p (t d) -> p t d", t=STORE_TILES),
                 )
+
+        def cell_state(j, t):
+            cols = slice(t * D, (t + 1) * D)
+            forget_rows = gate_by_row(forget[j], t)
+            nc.vector.tensor_tensor(out=c_new[j][:, cols], in0=forget_rows[:], in1=c_rows[j][:, cols], op=ALU.mult)
+            nc.gpsimd.tensor_tensor(out=c_new[j][:, cols], in0=c_new[j][:, cols], in1=cand_rows[j][:, cols], op=ALU.add)
+            store(c_out, j, t, c_new[j])
+
+        def tanh_of_cell_state(j, t):
+            cols = slice(t * D, (t + 1) * D)
+            nc.scalar.activation(out=tanh_c[j][:, cols], in_=c_new[j][:, cols], func=ACT.Tanh)
+
+        def hidden_state(j, t):
+            cols = slice(t * D, (t + 1) * D)
+            output_rows = gate_by_row(output[j], t)
+            nc.vector.tensor_tensor(out=h_new[j][:, cols], in0=output_rows[:], in1=tanh_c[j][:, cols], op=ALU.mult)
+            store(h_out, j, t, h_new[j])
 
         ident = const.tile([P, P], F32, name="ident")
         make_identity(nc, ident[:])
@@ -161,10 +182,10 @@ def tile_lstmcell_pb_t_kernel(
             )
 
         x_q, h_q = {}, {}
-        w_f_q = quantise(k_to_partitions(w_f_rows, True), const, "W_f")
-        u_f_q = quantise(k_to_partitions(u_f_rows, True), const, "U_f")
-        x_q[0] = quantise(k_to_partitions(x_rows[0], True), mxops, "x")
-        h_q[0] = quantise(k_to_partitions(h_rows[0], True), mxops, "h")
+        w_f_q = prepare(w_f_rows, const, "W_f")
+        u_f_q = prepare(u_f_rows, const, "U_f")
+        x_q[0] = prepare(x_rows[0], mxops, "x")
+        h_q[0] = prepare(h_rows[0], mxops, "h")
 
         bias_rows_f32 = const.tile([P, P], F32, name="bias_rows_f32")
         nc.vector.tensor_copy(out=bias_rows_f32[:], in_=bias_rows[:])
@@ -181,47 +202,55 @@ def tile_lstmcell_pb_t_kernel(
         )
         FORGET_BIAS, OUTPUT_BIAS = 0, FEATURE_TILES
 
-        for j in range(CHUNKS):
+        forget, output, c_new, tanh_c, h_new, x_grouped, h_grouped = {}, {}, {}, {}, {}, {}, {}
+        for j in range(CHUNKS + 1):
             if j + LOADS_AHEAD < CHUNKS:
                 load_acts(j + LOADS_AHEAD)
                 load_state(j + LOADS_AHEAD)
 
-            forget = gate_by_feature(w_f_q, u_f_q, x_q[j], h_q[j], FORGET_BIAS, "forget")
-
+            if j < CHUNKS:
+                forget[j] = gates.tile([P, FEATURE_TILES * CHUNK_ROWS], F32, name="forget", tag="forget")
+                half_gate(forget[j], 0, w_f_q, u_f_q, j, FORGET_BIAS)
             if j == 0:
-                w_o_q = quantise(k_to_partitions(w_o_rows, True), const, "W_o")
-                u_o_q = quantise(k_to_partitions(u_o_rows, True), const, "U_o")
-                x_q[1] = quantise(k_to_partitions(x_rows[1], True), mxops, "x")
+                w_o_q = prepare(w_o_rows, const, "W_o")
+                u_o_q = prepare(u_o_rows, const, "U_o")
+            else:
+                tanh_of_cell_state(j - 1, 2)
+                tanh_of_cell_state(j - 1, 3)
+                h_new[j - 1] = outs.tile([P, TILES * D], F32, name="h_new", tag="h_new")
+                for t in range(3):
+                    hidden_state(j - 1, t)
+
+            if j < CHUNKS:
+                half_gate(forget[j], 1, w_f_q, u_f_q, j, FORGET_BIAS)
+            if j == 0:
+                x_grouped[1] = new_grouped("x")
+                k_to_partitions(x_rows[1], x_grouped[1], 0, False)
+                k_to_partitions(x_rows[1], x_grouped[1], 1, True)
+            else:
+                hidden_state(j - 1, 3)
             if j + 1 < CHUNKS:
-                h_grouped = k_to_partitions(h_rows[j + 1], True)
+                h_grouped[j + 1] = new_grouped("h")
+                k_to_partitions(h_rows[j + 1], h_grouped[j + 1], 0, False)
+                k_to_partitions(h_rows[j + 1], h_grouped[j + 1], 1, True)
+                x_q[j + 1] = quantise(x_grouped[j + 1], mxops, "x")
+            if j == CHUNKS:
+                break
 
-            c_new = outs.tile([P, TILES * D], F32, name="c_new", tag="c_new")
-            for t in range(TILES):
-                cols = slice(t * D, (t + 1) * D)
-                forget_rows = gate_by_row(forget, t)
-                nc.vector.tensor_tensor(out=c_new[:, cols], in0=forget_rows[:], in1=c_rows[j][:, cols], op=ALU.mult)
-                nc.vector.tensor_tensor(out=c_new[:, cols], in0=c_new[:, cols], in1=cand_rows[j][:, cols], op=ALU.add)
-                store(c_out, j, t, c_new)
-
+            output[j] = gates.tile([P, FEATURE_TILES * CHUNK_ROWS], F32, name="output", tag="output")
+            half_gate(output[j], 0, w_o_q, u_o_q, j, OUTPUT_BIAS)
             if j + 1 < CHUNKS:
-                h_q[j + 1] = quantise(h_grouped, mxops, "h")
+                h_q[j + 1] = quantise(h_grouped[j + 1], mxops, "h")
+            c_new[j] = outs.tile([P, TILES * D], F32, name="c_new", tag="c_new")
+            for t in range(3):
+                cell_state(j, t)
 
-            output = gate_by_feature(w_o_q, u_o_q, x_q[j], h_q[j], OUTPUT_BIAS, "output")
-
-            tanh_c = outs.tile([P, TILES * D], F32, name="tanh_c", tag="tanh_c")
-            for t in range(TILES):
-                cols = slice(t * D, (t + 1) * D)
-                nc.scalar.activation(out=tanh_c[:, cols], in_=c_new[:, cols], func=ACT.Tanh)
-
+            half_gate(output[j], 1, w_o_q, u_o_q, j, OUTPUT_BIAS)
+            tanh_c[j] = outs.tile([P, TILES * D], F32, name="tanh_c", tag="tanh_c")
+            tanh_of_cell_state(j, 0)
+            tanh_of_cell_state(j, 1)
+            cell_state(j, 3)
             if j + 2 < CHUNKS:
-                x_grouped = k_to_partitions(x_rows[j + 2], False)
-
-            h_new = outs.tile([P, TILES * D], F32, name="h_new", tag="h_new")
-            for t in range(TILES):
-                cols = slice(t * D, (t + 1) * D)
-                output_rows = gate_by_row(output, t)
-                nc.vector.tensor_tensor(out=h_new[:, cols], in0=output_rows[:], in1=tanh_c[:, cols], op=ALU.mult)
-                store(h_out, j, t, h_new)
-
-            if j + 2 < CHUNKS:
-                x_q[j + 2] = quantise(x_grouped, mxops, "x")
+                x_grouped[j + 2] = new_grouped("x")
+                k_to_partitions(x_rows[j + 2], x_grouped[j + 2], 0, False)
+                k_to_partitions(x_rows[j + 2], x_grouped[j + 2], 1, False)

@@ -16,13 +16,13 @@ PACK = 4
 BATCH = 4096
 D = 512
 BANK = 512
-PSUM_BANKS = 8
+PSUM_TILES = 4
 ROW_TILES = BATCH // P
 TILES = 4
 CHUNK_ROWS = TILES * P
 CHUNKS = ROW_TILES // TILES
 FEATURE_TILES = D // P
-STORE_TILES = 2
+PAIR = 2
 LOADS_AHEAD = 3
 
 FLOPS = 4 * 2 * BATCH * D * D
@@ -47,7 +47,7 @@ def tile_lstmcell_pb_t_kernel(
         mxops = ctx.enter_context(tc.tile_pool(name="mxops", bufs=2))
         gates = ctx.enter_context(tc.tile_pool(name="gates", bufs=2))
         outs = ctx.enter_context(tc.tile_pool(name="outs", bufs=3))
-        banks = ctx.enter_context(tc.psum_pool(name="banks", bufs=PSUM_BANKS))
+        banks = ctx.enter_context(tc.psum_pool(name="banks", bufs=PSUM_TILES))
         ctx.enter_context(tc.manual_schedule())
 
         def load(view, first_tile, pool, tag):
@@ -58,22 +58,25 @@ def tile_lstmcell_pb_t_kernel(
             )
             return rows
 
-        def new_grouped(tag):
-            return stage.tile([P, TILES * P * PACK], BF16, name="grouped_" + tag, tag="grouped_" + tag, align_bytes=64)
+        def two_banks():
+            return banks.tile([P, PAIR * BANK], F32, name="two_banks", tag="two_banks")
 
-        def k_to_partitions(rows, grouped, pair, on_scalar):
+        def k_to_partitions(rows, tag, scalar_helps):
+            grouped = stage.tile([P, TILES * P * PACK], BF16, name="grouped_" + tag, tag="grouped_" + tag, align_bytes=64)
             row_words = rows[:].bitcast(F32).rearrange("r (t u q) -> r t u q", t=TILES, u=2)
             grouped_words = grouped[:].bitcast(F32).rearrange("q (t r u) -> q t r u", t=TILES, u=2)
-            bank = banks.tile([P, BANK], F32, name="bank", tag="bank")
-            turned = bank[:].rearrange("q (i u r) -> q i u r", i=2, u=2)
-            for i in range(2):
+            turned = two_banks()[:].rearrange("q (t u r) -> q t u r", t=TILES, u=2)
+            for t in range(TILES):
                 for u in range(2):
-                    nc.tensor.transpose(turned[:, i, u, :], row_words[:, 2 * pair + i, u, :], ident[:])
-            side_by_side = turned.rearrange("q i u r -> q i r u")
-            if on_scalar:
-                nc.scalar.copy(out=grouped_words[:, 2 * pair : 2 * pair + 2, :, :], in_=side_by_side)
-            else:
-                nc.vector.tensor_copy(out=grouped_words[:, 2 * pair : 2 * pair + 2, :, :], in_=side_by_side)
+                    nc.tensor.transpose(turned[:, t, u, :], row_words[:, t, u, :], ident[:])
+            for bank in range(PAIR):
+                tiles = slice(bank * PAIR, (bank + 1) * PAIR)
+                side_by_side = turned[:, tiles, :, :].rearrange("q t u r -> q t r u")
+                if scalar_helps and bank == 1:
+                    nc.scalar.copy(out=grouped_words[:, tiles, :, :], in_=side_by_side)
+                else:
+                    nc.vector.tensor_copy(out=grouped_words[:, tiles, :, :], in_=side_by_side)
+            return grouped
 
         def quantise(grouped, pool, tag):
             codes = pool.tile([P, TILES * P], U32, name="codes_" + tag, tag="codes_" + tag, align_bytes=64)
@@ -81,19 +84,14 @@ def tile_lstmcell_pb_t_kernel(
             nc.vector.quantize_mx(out=codes[:].bitcast(FP8X4), scales=scales[:], in_=grouped[:])
             return codes, scales
 
-        def prepare(rows, pool, tag):
-            grouped = new_grouped("first")
-            k_to_partitions(rows, grouped, 0, False)
-            k_to_partitions(rows, grouped, 1, True)
-            return quantise(grouped, pool, tag)
-
         def half_gate(gate, half, w_in, w_rec, j, first_bias):
-            for a in range(2 * half, 2 * half + 2):
+            acc = two_banks()
+            for bank in range(PAIR):
+                a = half * PAIR + bank
                 features = slice(a * P, (a + 1) * P)
-                acc = banks.tile([P, BANK], F32, name="bank", tag="bank")
                 for step, (weight, moving) in enumerate(((w_in, x_q[j]), (w_rec, h_q[j]))):
                     nc.tensor.matmul_mx(
-                        out=acc[:],
+                        out=acc[:, bank * BANK : (bank + 1) * BANK],
                         lhsT=weight[0][:, features].bitcast(FP8X4),
                         lhsT_scale=weight[1][:, features],
                         rhs=moving[0][:].bitcast(FP8X4),
@@ -103,43 +101,59 @@ def tile_lstmcell_pb_t_kernel(
                     )
                 nc.scalar.activation(
                     out=gate[:, a * CHUNK_ROWS : (a + 1) * CHUNK_ROWS],
-                    in_=acc[:],
+                    in_=acc[:, bank * BANK : (bank + 1) * BANK],
                     func=ACT.Sigmoid,
                     bias=gate_bias[:, first_bias + a : first_bias + a + 1],
                     scale=1.0,
                 )
 
-        def gate_by_row(gate, t):
-            bank = banks.tile([P, BANK], F32, name="bank", tag="bank")
-            for a in range(FEATURE_TILES):
-                first = a * CHUNK_ROWS + t * P
-                nc.tensor.transpose(bank[:, a * P : (a + 1) * P], gate[:, first : first + P], ident[:])
-            return bank
+        def gate_by_row(gate, half):
+            by_row = two_banks()
+            for bank in range(PAIR):
+                t = half * PAIR + bank
+                for a in range(FEATURE_TILES):
+                    nc.tensor.transpose(
+                        by_row[:, bank * BANK + a * P : bank * BANK + (a + 1) * P],
+                        gate[:, a * CHUNK_ROWS + t * P : a * CHUNK_ROWS + (t + 1) * P],
+                        ident[:],
+                    )
+            return by_row
 
-        def store(view, j, t, result):
-            if (t + 1) % STORE_TILES == 0:
-                first = t + 1 - STORE_TILES
-                nc.sync.dma_start(
-                    out=view[:, j * TILES + first : j * TILES + t + 1, :],
-                    in_=result[:, first * D : (t + 1) * D].rearrange("p (t d) -> p t d", t=STORE_TILES),
+        def store(view, j, half, result):
+            nc.sync.dma_start(
+                out=view[:, j * TILES + half * PAIR : j * TILES + (half + 1) * PAIR, :],
+                in_=result[:, half * PAIR * D : (half + 1) * PAIR * D].rearrange("p (t d) -> p t d", t=PAIR),
+            )
+
+        def cell_state(j, half):
+            forget_rows = gate_by_row(forget[j], half)
+            for bank in range(PAIR):
+                cols = slice((half * PAIR + bank) * D, (half * PAIR + bank + 1) * D)
+                nc.vector.tensor_tensor(
+                    out=c_new[j][:, cols],
+                    in0=forget_rows[:, bank * BANK : (bank + 1) * BANK],
+                    in1=c_rows[j][:, cols],
+                    op=ALU.mult,
                 )
+                nc.gpsimd.tensor_tensor(out=c_new[j][:, cols], in0=c_new[j][:, cols], in1=cand_rows[j][:, cols], op=ALU.add)
+            store(c_out, j, half, c_new[j])
 
-        def cell_state(j, t):
-            cols = slice(t * D, (t + 1) * D)
-            forget_rows = gate_by_row(forget[j], t)
-            nc.vector.tensor_tensor(out=c_new[j][:, cols], in0=forget_rows[:], in1=c_rows[j][:, cols], op=ALU.mult)
-            nc.gpsimd.tensor_tensor(out=c_new[j][:, cols], in0=c_new[j][:, cols], in1=cand_rows[j][:, cols], op=ALU.add)
-            store(c_out, j, t, c_new[j])
+        def tanh_of_cell_state(j, half):
+            for t in range(half * PAIR, (half + 1) * PAIR):
+                cols = slice(t * D, (t + 1) * D)
+                nc.scalar.activation(out=tanh_c[j][:, cols], in_=c_new[j][:, cols], func=ACT.Tanh)
 
-        def tanh_of_cell_state(j, t):
-            cols = slice(t * D, (t + 1) * D)
-            nc.scalar.activation(out=tanh_c[j][:, cols], in_=c_new[j][:, cols], func=ACT.Tanh)
-
-        def hidden_state(j, t):
-            cols = slice(t * D, (t + 1) * D)
-            output_rows = gate_by_row(output[j], t)
-            nc.vector.tensor_tensor(out=h_new[j][:, cols], in0=output_rows[:], in1=tanh_c[j][:, cols], op=ALU.mult)
-            store(h_out, j, t, h_new[j])
+        def hidden_state(j, half):
+            output_rows = gate_by_row(output[j], half)
+            for bank in range(PAIR):
+                cols = slice((half * PAIR + bank) * D, (half * PAIR + bank + 1) * D)
+                nc.vector.tensor_tensor(
+                    out=h_new[j][:, cols],
+                    in0=output_rows[:, bank * BANK : (bank + 1) * BANK],
+                    in1=tanh_c[j][:, cols],
+                    op=ALU.mult,
+                )
+            store(h_out, j, half, h_new[j])
 
         ident = const.tile([P, P], F32, name="ident")
         make_identity(nc, ident[:])
@@ -182,14 +196,14 @@ def tile_lstmcell_pb_t_kernel(
             )
 
         x_q, h_q = {}, {}
-        w_f_q = prepare(w_f_rows, const, "W_f")
-        u_f_q = prepare(u_f_rows, const, "U_f")
-        x_q[0] = prepare(x_rows[0], mxops, "x")
-        h_q[0] = prepare(h_rows[0], mxops, "h")
+        w_f_q = quantise(k_to_partitions(w_f_rows, "w", True), const, "W_f")
+        u_f_q = quantise(k_to_partitions(u_f_rows, "w", True), const, "U_f")
+        x_q[0] = quantise(k_to_partitions(x_rows[0], "x", True), mxops, "x")
+        h_q[0] = quantise(k_to_partitions(h_rows[0], "h", True), mxops, "h")
 
         bias_rows_f32 = const.tile([P, P], F32, name="bias_rows_f32")
         nc.vector.tensor_copy(out=bias_rows_f32[:], in_=bias_rows[:])
-        bias_bank = banks.tile([P, BANK], F32, name="bank", tag="bank")
+        bias_bank = two_banks()
         nc.tensor.transpose(bias_bank[:, 0:P], bias_rows_f32[:], ident[:])
         bias_columns = const.tile([P, 4 * FEATURE_TILES], F32, name="bias_columns")
         nc.vector.tensor_copy(out=bias_columns[:], in_=bias_bank[:, 0 : 4 * FEATURE_TILES])
@@ -202,7 +216,7 @@ def tile_lstmcell_pb_t_kernel(
         )
         FORGET_BIAS, OUTPUT_BIAS = 0, FEATURE_TILES
 
-        forget, output, c_new, tanh_c, h_new, x_grouped, h_grouped = {}, {}, {}, {}, {}, {}, {}
+        forget, output, c_new, tanh_c, h_new, x_grouped = {}, {}, {}, {}, {}, {}
         for j in range(CHUNKS + 1):
             if j + LOADS_AHEAD < CHUNKS:
                 load_acts(j + LOADS_AHEAD)
@@ -212,45 +226,33 @@ def tile_lstmcell_pb_t_kernel(
                 forget[j] = gates.tile([P, FEATURE_TILES * CHUNK_ROWS], F32, name="forget", tag="forget")
                 half_gate(forget[j], 0, w_f_q, u_f_q, j, FORGET_BIAS)
             if j == 0:
-                w_o_q = prepare(w_o_rows, const, "W_o")
-                u_o_q = prepare(u_o_rows, const, "U_o")
+                w_o_q = quantise(k_to_partitions(w_o_rows, "w", True), const, "W_o")
+                u_o_q = quantise(k_to_partitions(u_o_rows, "w", True), const, "U_o")
             else:
-                tanh_of_cell_state(j - 1, 2)
-                tanh_of_cell_state(j - 1, 3)
+                tanh_of_cell_state(j - 1, 1)
                 h_new[j - 1] = outs.tile([P, TILES * D], F32, name="h_new", tag="h_new")
-                for t in range(3):
-                    hidden_state(j - 1, t)
-
-            if j < CHUNKS:
-                half_gate(forget[j], 1, w_f_q, u_f_q, j, FORGET_BIAS)
-            if j == 0:
-                x_grouped[1] = new_grouped("x")
-                k_to_partitions(x_rows[1], x_grouped[1], 0, False)
-                k_to_partitions(x_rows[1], x_grouped[1], 1, True)
-            else:
-                hidden_state(j - 1, 3)
-            if j + 1 < CHUNKS:
-                h_grouped[j + 1] = new_grouped("h")
-                k_to_partitions(h_rows[j + 1], h_grouped[j + 1], 0, False)
-                k_to_partitions(h_rows[j + 1], h_grouped[j + 1], 1, True)
-                x_q[j + 1] = quantise(x_grouped[j + 1], mxops, "x")
+                hidden_state(j - 1, 0)
+                hidden_state(j - 1, 1)
             if j == CHUNKS:
                 break
+
+            half_gate(forget[j], 1, w_f_q, u_f_q, j, FORGET_BIAS)
+            if j == 0:
+                x_grouped[1] = k_to_partitions(x_rows[1], "x", True)
+            if j + 1 < CHUNKS:
+                h_grouped = k_to_partitions(h_rows[j + 1], "h", True)
+                x_q[j + 1] = quantise(x_grouped[j + 1], mxops, "x")
 
             output[j] = gates.tile([P, FEATURE_TILES * CHUNK_ROWS], F32, name="output", tag="output")
             half_gate(output[j], 0, w_o_q, u_o_q, j, OUTPUT_BIAS)
             if j + 1 < CHUNKS:
-                h_q[j + 1] = quantise(h_grouped[j + 1], mxops, "h")
+                h_q[j + 1] = quantise(h_grouped, mxops, "h")
             c_new[j] = outs.tile([P, TILES * D], F32, name="c_new", tag="c_new")
-            for t in range(3):
-                cell_state(j, t)
+            cell_state(j, 0)
+            cell_state(j, 1)
 
             half_gate(output[j], 1, w_o_q, u_o_q, j, OUTPUT_BIAS)
             tanh_c[j] = outs.tile([P, TILES * D], F32, name="tanh_c", tag="tanh_c")
             tanh_of_cell_state(j, 0)
-            tanh_of_cell_state(j, 1)
-            cell_state(j, 3)
             if j + 2 < CHUNKS:
-                x_grouped[j + 2] = new_grouped("x")
-                k_to_partitions(x_rows[j + 2], x_grouped[j + 2], 0, False)
-                k_to_partitions(x_rows[j + 2], x_grouped[j + 2], 1, False)
+                x_grouped[j + 2] = k_to_partitions(x_rows[j + 2], "x", False)

@@ -16,13 +16,13 @@ PACK = 4
 BATCH = 4096
 D = 512
 BANK = 512
-PSUM_TILES = 4
+PSUM_BANKS = 8
 ROW_TILES = BATCH // P
 TILES = 4
 CHUNK_ROWS = TILES * P
 CHUNKS = ROW_TILES // TILES
 FEATURE_TILES = D // P
-PAIR = 2
+STORE_TILES = 2
 LOADS_AHEAD = 3
 
 FLOPS = 4 * 2 * BATCH * D * D
@@ -47,7 +47,7 @@ def tile_lstmcell_pb_t_kernel(
         mxops = ctx.enter_context(tc.tile_pool(name="mxops", bufs=2))
         gates = ctx.enter_context(tc.tile_pool(name="gates", bufs=2))
         outs = ctx.enter_context(tc.tile_pool(name="outs", bufs=3))
-        banks = ctx.enter_context(tc.psum_pool(name="banks", bufs=PSUM_TILES))
+        banks = ctx.enter_context(tc.psum_pool(name="banks", bufs=PSUM_BANKS))
         ctx.enter_context(tc.manual_schedule())
 
         def load(view, first_tile, pool, tag):
@@ -58,25 +58,22 @@ def tile_lstmcell_pb_t_kernel(
             )
             return rows
 
-        def two_banks():
-            return banks.tile([P, PAIR * BANK], F32, name="two_banks", tag="two_banks")
+        def new_grouped(tag):
+            return stage.tile([P, TILES * P * PACK], BF16, name="grouped_" + tag, tag="grouped_" + tag, align_bytes=64)
 
-        def k_to_partitions(rows, tag, scalar_helps):
-            grouped = stage.tile([P, TILES * P * PACK], BF16, name="grouped_" + tag, tag="grouped_" + tag, align_bytes=64)
+        def k_to_partitions(rows, grouped, pair, on_scalar):
             row_words = rows[:].bitcast(F32).rearrange("r (t u q) -> r t u q", t=TILES, u=2)
             grouped_words = grouped[:].bitcast(F32).rearrange("q (t r u) -> q t r u", t=TILES, u=2)
-            turned = two_banks()[:].rearrange("q (t u r) -> q t u r", t=TILES, u=2)
-            for t in range(TILES):
+            bank = banks.tile([P, BANK], F32, name="bank", tag="bank")
+            turned = bank[:].rearrange("q (i u r) -> q i u r", i=2, u=2)
+            for i in range(2):
                 for u in range(2):
-                    nc.tensor.transpose(turned[:, t, u, :], row_words[:, t, u, :], ident[:])
-            for bank in range(PAIR):
-                tiles = slice(bank * PAIR, (bank + 1) * PAIR)
-                side_by_side = turned[:, tiles, :, :].rearrange("q t u r -> q t r u")
-                if scalar_helps and bank == 1:
-                    nc.scalar.copy(out=grouped_words[:, tiles, :, :], in_=side_by_side)
-                else:
-                    nc.vector.tensor_copy(out=grouped_words[:, tiles, :, :], in_=side_by_side)
-            return grouped
+                    nc.tensor.transpose(turned[:, i, u, :], row_words[:, 2 * pair + i, u, :], ident[:])
+            side_by_side = turned.rearrange("q i u r -> q i r u")
+            if on_scalar:
+                nc.scalar.copy(out=grouped_words[:, 2 * pair : 2 * pair + 2, :, :], in_=side_by_side)
+            else:
+                nc.vector.tensor_copy(out=grouped_words[:, 2 * pair : 2 * pair + 2, :, :], in_=side_by_side)
 
         def quantise(grouped, pool, tag):
             codes = pool.tile([P, TILES * P], U32, name="codes_" + tag, tag="codes_" + tag, align_bytes=64)
@@ -84,14 +81,19 @@ def tile_lstmcell_pb_t_kernel(
             nc.vector.quantize_mx(out=codes[:].bitcast(FP8X4), scales=scales[:], in_=grouped[:])
             return codes, scales
 
+        def prepare(rows, pool, tag):
+            grouped = new_grouped("first")
+            k_to_partitions(rows, grouped, 0, False)
+            k_to_partitions(rows, grouped, 1, True)
+            return quantise(grouped, pool, tag)
+
         def half_gate(gate, half, w_in, w_rec, j, first_bias):
-            acc = two_banks()
-            for bank in range(PAIR):
-                a = half * PAIR + bank
+            for a in range(2 * half, 2 * half + 2):
                 features = slice(a * P, (a + 1) * P)
+                acc = banks.tile([P, BANK], F32, name="bank", tag="bank")
                 for step, (weight, moving) in enumerate(((w_in, x_q[j]), (w_rec, h_q[j]))):
                     nc.tensor.matmul_mx(
-                        out=acc[:, bank * BANK : (bank + 1) * BANK],
+                        out=acc[:],
                         lhsT=weight[0][:, features].bitcast(FP8X4),
                         lhsT_scale=weight[1][:, features],
                         rhs=moving[0][:].bitcast(FP8X4),
@@ -101,62 +103,56 @@ def tile_lstmcell_pb_t_kernel(
                     )
                 nc.scalar.activation(
                     out=gate[:, a * CHUNK_ROWS : (a + 1) * CHUNK_ROWS],
-                    in_=acc[:, bank * BANK : (bank + 1) * BANK],
+                    in_=acc[:],
                     func=ACT.Sigmoid,
                     bias=gate_bias[:, first_bias + a : first_bias + a + 1],
                     scale=1.0,
                 )
 
-        def gate_by_row(gate, half):
-            by_row = two_banks()
-            for bank in range(PAIR):
-                t = half * PAIR + bank
-                for a in range(FEATURE_TILES):
-                    nc.tensor.transpose(
-                        by_row[:, bank * BANK + a * P : bank * BANK + (a + 1) * P],
-                        gate[:, a * CHUNK_ROWS + t * P : a * CHUNK_ROWS + (t + 1) * P],
-                        ident[:],
-                    )
-            return by_row
+        def gate_by_row(gate, t):
+            bank = banks.tile([P, BANK], F32, name="bank", tag="bank")
+            for a in range(FEATURE_TILES):
+                first = a * CHUNK_ROWS + t * P
+                nc.tensor.transpose(bank[:, a * P : (a + 1) * P], gate[:, first : first + P], ident[:])
+            return bank
 
-        def store(view, j, half, result):
-            nc.sync.dma_start(
-                out=view[:, j * TILES + half * PAIR : j * TILES + (half + 1) * PAIR, :],
-                in_=result[:, half * PAIR * D : (half + 1) * PAIR * D].rearrange("p (t d) -> p t d", t=PAIR),
+        def store(view, j, t, result):
+            if (t + 1) % STORE_TILES == 0:
+                first = t + 1 - STORE_TILES
+                nc.sync.dma_start(
+                    out=view[:, j * TILES + first : j * TILES + t + 1, :],
+                    in_=result[:, first * D : (t + 1) * D].rearrange("p (t d) -> p t d", t=STORE_TILES),
+                )
+
+        def cell_state(j, t):
+            cols = slice(t * D, (t + 1) * D)
+            forget_rows = gate_by_row(forget[j], t)
+            nc.vector.tensor_tensor(out=c_new[j][:, cols], in0=forget_rows[:], in1=c_rows[j][:, cols], op=ALU.mult)
+            nc.gpsimd.tensor_tensor(out=c_new[j][:, cols], in0=c_new[j][:, cols], in1=cand_rows[j][:, cols], op=ALU.add)
+            store(c_out, j, t, c_new[j])
+
+        def tanh_of_cell_state(j, t):
+            cols = slice(t * D, (t + 1) * D)
+            nc.scalar.activation(out=tanh_c[j][:, cols], in_=c_new[j][:, cols], func=ACT.Tanh)
+
+        def hidden_state(j, t):
+            cols = slice(t * D, (t + 1) * D)
+            output_rows = gate_by_row(output[j], t)
+            nc.vector.tensor_tensor(out=h_new[j][:, cols], in0=output_rows[:], in1=tanh_c[j][:, cols], op=ALU.mult)
+            store(h_out, j, t, h_new[j])
+
+        bias_rows = const.tile([P, P], BF16, name="bias_rows")
+        nc.gpsimd.memset(bias_rows[:], 0.0)
+        for v, vector in enumerate((b_W_f, b_W_o, b_U_f, b_U_o)):
+            nc.scalar.dma_start(
+                out=bias_rows[v * FEATURE_TILES : (v + 1) * FEATURE_TILES, :],
+                in_=vector.rearrange("(a p) -> a p", p=P),
             )
-
-        def cell_state(j, half):
-            forget_rows = gate_by_row(forget[j], half)
-            for bank in range(PAIR):
-                cols = slice((half * PAIR + bank) * D, (half * PAIR + bank + 1) * D)
-                nc.vector.tensor_tensor(
-                    out=c_new[j][:, cols],
-                    in0=forget_rows[:, bank * BANK : (bank + 1) * BANK],
-                    in1=c_rows[j][:, cols],
-                    op=ALU.mult,
-                )
-                nc.gpsimd.tensor_tensor(out=c_new[j][:, cols], in0=c_new[j][:, cols], in1=cand_rows[j][:, cols], op=ALU.add)
-            store(c_out, j, half, c_new[j])
-
-        def tanh_of_cell_state(j, half):
-            for t in range(half * PAIR, (half + 1) * PAIR):
-                cols = slice(t * D, (t + 1) * D)
-                nc.scalar.activation(out=tanh_c[j][:, cols], in_=c_new[j][:, cols], func=ACT.Tanh)
-
-        def hidden_state(j, half):
-            output_rows = gate_by_row(output[j], half)
-            for bank in range(PAIR):
-                cols = slice((half * PAIR + bank) * D, (half * PAIR + bank + 1) * D)
-                nc.vector.tensor_tensor(
-                    out=h_new[j][:, cols],
-                    in0=output_rows[:, bank * BANK : (bank + 1) * BANK],
-                    in1=tanh_c[j][:, cols],
-                    op=ALU.mult,
-                )
-            store(h_out, j, half, h_new[j])
 
         ident = const.tile([P, P], F32, name="ident")
         make_identity(nc, ident[:])
+        ident_bf16 = const.tile([P, P], BF16, name="ident_bf16")
+        make_identity(nc, ident_bf16[:])
 
         zero = const.tile([P, 1], F32, name="zero")
         nc.vector.memset(zero[:], 0.0)
@@ -187,24 +183,14 @@ def tile_lstmcell_pb_t_kernel(
         load_state(1)
         load_state(2)
 
-        bias_rows = const.tile([P, P], BF16, name="bias_rows")
-        nc.gpsimd.memset(bias_rows[:], 0.0)
-        for v, vector in enumerate((b_W_f, b_W_o, b_U_f, b_U_o)):
-            nc.scalar.dma_start(
-                out=bias_rows[v * FEATURE_TILES : (v + 1) * FEATURE_TILES, :],
-                in_=vector.rearrange("(a p) -> a p", p=P),
-            )
-
         x_q, h_q = {}, {}
-        w_f_q = quantise(k_to_partitions(w_f_rows, "w", True), const, "W_f")
-        u_f_q = quantise(k_to_partitions(u_f_rows, "w", True), const, "U_f")
-        x_q[0] = quantise(k_to_partitions(x_rows[0], "x", True), mxops, "x")
-        h_q[0] = quantise(k_to_partitions(h_rows[0], "h", True), mxops, "h")
+        w_f_q = prepare(w_f_rows, const, "W_f")
+        u_f_q = prepare(u_f_rows, const, "U_f")
+        x_q[0] = prepare(x_rows[0], mxops, "x")
+        h_q[0] = prepare(h_rows[0], mxops, "h")
 
-        bias_rows_f32 = const.tile([P, P], F32, name="bias_rows_f32")
-        nc.vector.tensor_copy(out=bias_rows_f32[:], in_=bias_rows[:])
-        bias_bank = two_banks()
-        nc.tensor.transpose(bias_bank[:, 0:P], bias_rows_f32[:], ident[:])
+        bias_bank = banks.tile([P, 2 * BANK], BF16, name="bank", tag="bank")
+        nc.tensor.transpose(bias_bank[:, 0:P], bias_rows[:], ident_bf16[:])
         bias_columns = const.tile([P, 4 * FEATURE_TILES], F32, name="bias_columns")
         nc.vector.tensor_copy(out=bias_columns[:], in_=bias_bank[:, 0 : 4 * FEATURE_TILES])
         gate_bias = const.tile([P, 2 * FEATURE_TILES], F32, name="gate_bias")
@@ -216,7 +202,7 @@ def tile_lstmcell_pb_t_kernel(
         )
         FORGET_BIAS, OUTPUT_BIAS = 0, FEATURE_TILES
 
-        forget, output, c_new, tanh_c, h_new, x_grouped = {}, {}, {}, {}, {}, {}
+        forget, output, c_new, tanh_c, h_new, x_grouped, h_grouped = {}, {}, {}, {}, {}, {}, {}
         for j in range(CHUNKS + 1):
             if j + LOADS_AHEAD < CHUNKS:
                 load_acts(j + LOADS_AHEAD)
@@ -226,33 +212,45 @@ def tile_lstmcell_pb_t_kernel(
                 forget[j] = gates.tile([P, FEATURE_TILES * CHUNK_ROWS], F32, name="forget", tag="forget")
                 half_gate(forget[j], 0, w_f_q, u_f_q, j, FORGET_BIAS)
             if j == 0:
-                w_o_q = quantise(k_to_partitions(w_o_rows, "w", True), const, "W_o")
-                u_o_q = quantise(k_to_partitions(u_o_rows, "w", True), const, "U_o")
+                w_o_q = prepare(w_o_rows, const, "W_o")
+                u_o_q = prepare(u_o_rows, const, "U_o")
             else:
-                tanh_of_cell_state(j - 1, 1)
+                tanh_of_cell_state(j - 1, 2)
+                tanh_of_cell_state(j - 1, 3)
                 h_new[j - 1] = outs.tile([P, TILES * D], F32, name="h_new", tag="h_new")
-                hidden_state(j - 1, 0)
-                hidden_state(j - 1, 1)
+                for t in range(3):
+                    hidden_state(j - 1, t)
+
+            if j < CHUNKS:
+                half_gate(forget[j], 1, w_f_q, u_f_q, j, FORGET_BIAS)
+            if j == 0:
+                x_grouped[1] = new_grouped("x")
+                k_to_partitions(x_rows[1], x_grouped[1], 0, False)
+                k_to_partitions(x_rows[1], x_grouped[1], 1, True)
+            else:
+                hidden_state(j - 1, 3)
+            if j + 1 < CHUNKS:
+                h_grouped[j + 1] = new_grouped("h")
+                k_to_partitions(h_rows[j + 1], h_grouped[j + 1], 0, False)
+                k_to_partitions(h_rows[j + 1], h_grouped[j + 1], 1, True)
+                x_q[j + 1] = quantise(x_grouped[j + 1], mxops, "x")
             if j == CHUNKS:
                 break
-
-            half_gate(forget[j], 1, w_f_q, u_f_q, j, FORGET_BIAS)
-            if j == 0:
-                x_grouped[1] = k_to_partitions(x_rows[1], "x", True)
-            if j + 1 < CHUNKS:
-                h_grouped = k_to_partitions(h_rows[j + 1], "h", True)
-                x_q[j + 1] = quantise(x_grouped[j + 1], mxops, "x")
 
             output[j] = gates.tile([P, FEATURE_TILES * CHUNK_ROWS], F32, name="output", tag="output")
             half_gate(output[j], 0, w_o_q, u_o_q, j, OUTPUT_BIAS)
             if j + 1 < CHUNKS:
-                h_q[j + 1] = quantise(h_grouped, mxops, "h")
+                h_q[j + 1] = quantise(h_grouped[j + 1], mxops, "h")
             c_new[j] = outs.tile([P, TILES * D], F32, name="c_new", tag="c_new")
-            cell_state(j, 0)
-            cell_state(j, 1)
+            for t in range(3):
+                cell_state(j, t)
 
             half_gate(output[j], 1, w_o_q, u_o_q, j, OUTPUT_BIAS)
             tanh_c[j] = outs.tile([P, TILES * D], F32, name="tanh_c", tag="tanh_c")
             tanh_of_cell_state(j, 0)
+            tanh_of_cell_state(j, 1)
+            cell_state(j, 3)
             if j + 2 < CHUNKS:
-                x_grouped[j + 2] = k_to_partitions(x_rows[j + 2], "x", False)
+                x_grouped[j + 2] = new_grouped("x")
+                k_to_partitions(x_rows[j + 2], x_grouped[j + 2], 0, False)
+                k_to_partitions(x_rows[j + 2], x_grouped[j + 2], 1, False)

@@ -44,7 +44,7 @@ def tile_lstmcell_pb_t_kernel(
         acts = ctx.enter_context(tc.tile_pool(name="acts", bufs=LOADS_AHEAD))
         state = ctx.enter_context(tc.tile_pool(name="state", bufs=LOADS_AHEAD + 1))
         stage = ctx.enter_context(tc.tile_pool(name="stage", bufs=2))
-        mxops = ctx.enter_context(tc.tile_pool(name="mxops", bufs=2))
+        mxops = ctx.enter_context(tc.tile_pool(name="mxops", bufs=3))
         gates = ctx.enter_context(tc.tile_pool(name="gates", bufs=2))
         outs = ctx.enter_context(tc.tile_pool(name="outs", bufs=3))
         banks = ctx.enter_context(tc.psum_pool(name="banks", bufs=PSUM_BANKS))
@@ -116,8 +116,10 @@ def tile_lstmcell_pb_t_kernel(
                 nc.tensor.transpose(bank[:, a * P : (a + 1) * P], gate[:, first : first + P], ident[:])
             return bank
 
-        def store(view, j, t, result):
-            if (t + 1) % STORE_TILES == 0:
+        def store(view, j, t, result, alone=False):
+            if alone:
+                nc.sync.dma_start(out=view[:, j * TILES + t, :], in_=result[:, t * D : (t + 1) * D])
+            elif (t + 1) % STORE_TILES == 0:
                 first = t + 1 - STORE_TILES
                 nc.sync.dma_start(
                     out=view[:, j * TILES + first : j * TILES + t + 1, :],
@@ -129,7 +131,7 @@ def tile_lstmcell_pb_t_kernel(
             forget_rows = gate_by_row(forget[j], t)
             nc.vector.tensor_tensor(out=c_new[j][:, cols], in0=forget_rows[:], in1=c_rows[j][:, cols], op=ALU.mult)
             nc.gpsimd.tensor_tensor(out=c_new[j][:, cols], in0=c_new[j][:, cols], in1=cand_rows[j][:, cols], op=ALU.add)
-            store(c_out, j, t, c_new[j])
+            store(c_out, j, t, c_new[j], alone=(j == CHUNKS - 1))
 
         def tanh_of_cell_state(j, t):
             cols = slice(t * D, (t + 1) * D)
@@ -139,7 +141,7 @@ def tile_lstmcell_pb_t_kernel(
             cols = slice(t * D, (t + 1) * D)
             output_rows = gate_by_row(output[j], t)
             nc.vector.tensor_tensor(out=h_new[j][:, cols], in0=output_rows[:], in1=tanh_c[j][:, cols], op=ALU.mult)
-            store(h_out, j, t, h_new[j])
+            store(h_out, j, t, h_new[j], alone=(j == CHUNKS - 1))
 
         bias_rows = const.tile([P, P], BF16, name="bias_rows")
         nc.gpsimd.memset(bias_rows[:], 0.0)
@@ -175,15 +177,16 @@ def tile_lstmcell_pb_t_kernel(
         w_f_rows = load(by_feature_tile(W_f), 0, const, "W_f")
         u_f_rows = load(by_feature_tile(U_f), 0, const, "U_f")
         load_acts(0)
+        load_acts(1)
         w_o_rows = load(by_feature_tile(W_o), 0, const, "W_o")
         u_o_rows = load(by_feature_tile(U_o), 0, const, "U_o")
-        load_acts(1)
         load_state(0)
         load_acts(2)
         load_state(1)
         load_state(2)
 
         x_q, h_q = {}, {}
+        forget, output, c_new, tanh_c, h_new, x_grouped, h_grouped = {}, {}, {}, {}, {}, {}, {}
         w_f_q = prepare(w_f_rows, const, "W_f")
         u_f_q = prepare(u_f_rows, const, "U_f")
         x_q[0] = prepare(x_rows[0], mxops, "x")
@@ -201,56 +204,88 @@ def tile_lstmcell_pb_t_kernel(
             op=ALU.add,
         )
         FORGET_BIAS, OUTPUT_BIAS = 0, FEATURE_TILES
+        x_grouped[1] = new_grouped("x")
+        k_to_partitions(x_rows[1], x_grouped[1], 0, False)
+        k_to_partitions(x_rows[1], x_grouped[1], 1, True)
 
-        forget, output, c_new, tanh_c, h_new, x_grouped, h_grouped = {}, {}, {}, {}, {}, {}, {}
-        for j in range(CHUNKS + 1):
-            if j + LOADS_AHEAD < CHUNKS:
-                load_acts(j + LOADS_AHEAD)
-                load_state(j + LOADS_AHEAD)
+        for p in range(CHUNKS + 2):
+            if 0 < p and p + LOADS_AHEAD - 1 < CHUNKS:
+                load_acts(p + LOADS_AHEAD - 1)
+                load_state(p + LOADS_AHEAD - 1)
 
-            if j < CHUNKS:
-                forget[j] = gates.tile([P, FEATURE_TILES * CHUNK_ROWS], F32, name="forget", tag="forget")
-                half_gate(forget[j], 0, w_f_q, u_f_q, j, FORGET_BIAS)
-            if j == 0:
-                w_o_q = prepare(w_o_rows, const, "W_o")
-                u_o_q = prepare(u_o_rows, const, "U_o")
-            else:
-                tanh_of_cell_state(j - 1, 2)
-                tanh_of_cell_state(j - 1, 3)
-                h_new[j - 1] = outs.tile([P, TILES * D], F32, name="h_new", tag="h_new")
+            if p < CHUNKS:
+                forget[p] = gates.tile([P, FEATURE_TILES * CHUNK_ROWS], F32, name="forget", tag="forget")
+                half_gate(forget[p], 0, w_f_q, u_f_q, p, FORGET_BIAS)
+            if p == CHUNKS:
+                output[p - 1] = gates.tile([P, FEATURE_TILES * CHUNK_ROWS], F32, name="output", tag="output")
+                half_gate(output[p - 1], 0, w_o_q, u_o_q, p - 1, OUTPUT_BIAS)
+            if p == 0:
+                h_grouped[1] = new_grouped("h")
+                k_to_partitions(h_rows[1], h_grouped[1], 0, False)
+                k_to_partitions(h_rows[1], h_grouped[1], 1, True)
+                x_q[1] = quantise(x_grouped[1], mxops, "x")
+                w_o_grouped = new_grouped("first")
+                k_to_partitions(w_o_rows, w_o_grouped, 0, False)
+            if p == 1:
+                c_new[0] = outs.tile([P, TILES * D], F32, name="c_new", tag="c_new")
                 for t in range(3):
-                    hidden_state(j - 1, t)
+                    cell_state(0, t)
+                x_grouped[2] = new_grouped("x")
+                k_to_partitions(x_rows[2], x_grouped[2], 0, True)
+            if 2 <= p < CHUNKS:
+                tanh_of_cell_state(p - 1, 2)
+                tanh_of_cell_state(p - 1, 3)
+            if p >= 2:
+                h_new[p - 2] = outs.tile([P, TILES * D], F32, name="h_new", tag="h_new")
+                for t in range(2 if p == CHUNKS else 3):
+                    hidden_state(p - 2, t)
 
-            if j < CHUNKS:
-                half_gate(forget[j], 1, w_f_q, u_f_q, j, FORGET_BIAS)
-            if j == 0:
-                x_grouped[1] = new_grouped("x")
-                k_to_partitions(x_rows[1], x_grouped[1], 0, False)
-                k_to_partitions(x_rows[1], x_grouped[1], 1, True)
-            else:
-                hidden_state(j - 1, 3)
-            if j + 1 < CHUNKS:
-                h_grouped[j + 1] = new_grouped("h")
-                k_to_partitions(h_rows[j + 1], h_grouped[j + 1], 0, False)
-                k_to_partitions(h_rows[j + 1], h_grouped[j + 1], 1, True)
-                x_q[j + 1] = quantise(x_grouped[j + 1], mxops, "x")
-            if j == CHUNKS:
-                break
+            if p < CHUNKS:
+                half_gate(forget[p], 1, w_f_q, u_f_q, p, FORGET_BIAS)
+            if p == CHUNKS:
+                half_gate(output[p - 1], 1, w_o_q, u_o_q, p - 1, OUTPUT_BIAS)
+                tanh_of_cell_state(p - 1, 2)
+                tanh_of_cell_state(p - 1, 3)
+                hidden_state(p - 2, 2)
+            if p == 0:
+                k_to_partitions(w_o_rows, w_o_grouped, 1, True)
+                h_q[1] = quantise(h_grouped[1], mxops, "h")
+                w_o_q = quantise(w_o_grouped, const, "W_o")
+                u_o_q = prepare(u_o_rows, const, "U_o")
+                continue
+            if p == 1:
+                tanh_c[0] = outs.tile([P, TILES * D], F32, name="tanh_c", tag="tanh_c")
+                tanh_of_cell_state(0, 0)
+                tanh_of_cell_state(0, 1)
+                cell_state(0, 3)
+                k_to_partitions(x_rows[2], x_grouped[2], 1, True)
+            if p >= 2:
+                hidden_state(p - 2, 3)
+            if p + 1 < CHUNKS:
+                h_grouped[p + 1] = new_grouped("h")
+                k_to_partitions(h_rows[p + 1], h_grouped[p + 1], 0, False)
+                k_to_partitions(h_rows[p + 1], h_grouped[p + 1], 1, True)
+                x_q[p + 1] = quantise(x_grouped[p + 1], mxops, "x")
+            if p >= CHUNKS:
+                continue
 
-            output[j] = gates.tile([P, FEATURE_TILES * CHUNK_ROWS], F32, name="output", tag="output")
-            half_gate(output[j], 0, w_o_q, u_o_q, j, OUTPUT_BIAS)
-            if j + 1 < CHUNKS:
-                h_q[j + 1] = quantise(h_grouped[j + 1], mxops, "h")
-            c_new[j] = outs.tile([P, TILES * D], F32, name="c_new", tag="c_new")
+            output[p - 1] = gates.tile([P, FEATURE_TILES * CHUNK_ROWS], F32, name="output", tag="output")
+            half_gate(output[p - 1], 0, w_o_q, u_o_q, p - 1, OUTPUT_BIAS)
+            if p == 1:
+                tanh_of_cell_state(0, 2)
+                tanh_of_cell_state(0, 3)
+            if p + 1 < CHUNKS:
+                h_q[p + 1] = quantise(h_grouped[p + 1], mxops, "h")
+            c_new[p] = outs.tile([P, TILES * D], F32, name="c_new", tag="c_new")
             for t in range(3):
-                cell_state(j, t)
+                cell_state(p, t)
 
-            half_gate(output[j], 1, w_o_q, u_o_q, j, OUTPUT_BIAS)
-            tanh_c[j] = outs.tile([P, TILES * D], F32, name="tanh_c", tag="tanh_c")
-            tanh_of_cell_state(j, 0)
-            tanh_of_cell_state(j, 1)
-            cell_state(j, 3)
-            if j + 2 < CHUNKS:
-                x_grouped[j + 2] = new_grouped("x")
-                k_to_partitions(x_rows[j + 2], x_grouped[j + 2], 0, False)
-                k_to_partitions(x_rows[j + 2], x_grouped[j + 2], 1, False)
+            half_gate(output[p - 1], 1, w_o_q, u_o_q, p - 1, OUTPUT_BIAS)
+            tanh_c[p] = outs.tile([P, TILES * D], F32, name="tanh_c", tag="tanh_c")
+            tanh_of_cell_state(p, 0)
+            tanh_of_cell_state(p, 1)
+            cell_state(p, 3)
+            if p + 2 < CHUNKS:
+                x_grouped[p + 2] = new_grouped("x")
+                k_to_partitions(x_rows[p + 2], x_grouped[p + 2], 0, False)
+                k_to_partitions(x_rows[p + 2], x_grouped[p + 2], 1, False)

@@ -88,7 +88,10 @@ def tile_lstmcell_pb_t_kernel(
             return quantise(grouped, pool, tag)
 
         def half_gate(gate, half, w_in, w_rec, j, first_bias):
-            for a in range(2 * half, 2 * half + 2):
+            gate_tiles(gate, range(2 * half, 2 * half + 2), w_in, w_rec, j, first_bias)
+
+        def gate_tiles(gate, tiles, w_in, w_rec, j, first_bias):
+            for a in tiles:
                 features = slice(a * P, (a + 1) * P)
                 acc = banks.tile([P, BANK], F32, name="bank", tag="bank")
                 for step, (weight, moving) in enumerate(((w_in, x_q[j]), (w_rec, h_q[j]))):
@@ -209,83 +212,108 @@ def tile_lstmcell_pb_t_kernel(
         k_to_partitions(x_rows[1], x_grouped[1], 1, True)
 
         for p in range(CHUNKS + 2):
+            if p == 1:
+                load_acts(3)
+            if 0 < p and p + LOADS_AHEAD < CHUNKS:
+                load_acts(p + LOADS_AHEAD)
             if 0 < p and p + LOADS_AHEAD - 1 < CHUNKS:
-                load_acts(p + LOADS_AHEAD - 1)
                 load_state(p + LOADS_AHEAD - 1)
 
-            if p < CHUNKS:
+            if p < 2:
                 forget[p] = gates.tile([P, FEATURE_TILES * CHUNK_ROWS], F32, name="forget", tag="forget")
                 half_gate(forget[p], 0, w_f_q, u_f_q, p, FORGET_BIAS)
-            if p == CHUNKS:
-                output[p - 1] = gates.tile([P, FEATURE_TILES * CHUNK_ROWS], F32, name="output", tag="output")
-                half_gate(output[p - 1], 0, w_o_q, u_o_q, p - 1, OUTPUT_BIAS)
-            if p == 0:
-                h_grouped[1] = new_grouped("h")
-                k_to_partitions(h_rows[1], h_grouped[1], 0, False)
-                k_to_partitions(h_rows[1], h_grouped[1], 1, True)
-                x_q[1] = quantise(x_grouped[1], mxops, "x")
-                w_o_grouped = new_grouped("first")
-                k_to_partitions(w_o_rows, w_o_grouped, 0, False)
-            if p == 1:
-                c_new[0] = outs.tile([P, TILES * D], F32, name="c_new", tag="c_new")
-                for t in range(3):
-                    cell_state(0, t)
-                x_grouped[2] = new_grouped("x")
-                k_to_partitions(x_rows[2], x_grouped[2], 0, True)
-            if 2 <= p < CHUNKS:
-                tanh_of_cell_state(p - 1, 2)
-                tanh_of_cell_state(p - 1, 3)
-            if p >= 2:
-                h_new[p - 2] = outs.tile([P, TILES * D], F32, name="h_new", tag="h_new")
-                for t in range(2 if p == CHUNKS else 3):
-                    hidden_state(p - 2, t)
+                if p == 0:
+                    h_grouped[1] = new_grouped("h")
+                    k_to_partitions(h_rows[1], h_grouped[1], 0, False)
+                    k_to_partitions(h_rows[1], h_grouped[1], 1, True)
+                    x_q[1] = quantise(x_grouped[1], mxops, "x")
+                    w_o_grouped = new_grouped("first")
+                    k_to_partitions(w_o_rows, w_o_grouped, 0, False)
+                if p == 1:
+                    c_new[0] = outs.tile([P, TILES * D], F32, name="c_new", tag="c_new")
+                    for t in range(3):
+                        cell_state(0, t)
+                    x_grouped[2] = new_grouped("x")
+                    k_to_partitions(x_rows[2], x_grouped[2], 0, True)
 
-            if p < CHUNKS:
                 half_gate(forget[p], 1, w_f_q, u_f_q, p, FORGET_BIAS)
-            if p == CHUNKS:
-                half_gate(output[p - 1], 1, w_o_q, u_o_q, p - 1, OUTPUT_BIAS)
-                tanh_of_cell_state(p - 1, 2)
-                tanh_of_cell_state(p - 1, 3)
-                hidden_state(p - 2, 2)
-            if p == 0:
-                k_to_partitions(w_o_rows, w_o_grouped, 1, True)
-                h_q[1] = quantise(h_grouped[1], mxops, "h")
-                w_o_q = quantise(w_o_grouped, const, "W_o")
-                u_o_q = prepare(u_o_rows, const, "U_o")
-                continue
-            if p == 1:
+                if p == 0:
+                    k_to_partitions(w_o_rows, w_o_grouped, 1, True)
+                    h_q[1] = quantise(h_grouped[1], mxops, "h")
+                    w_o_q = quantise(w_o_grouped, const, "W_o")
+                    u_o_q = prepare(u_o_rows, const, "U_o")
+                    continue
                 tanh_c[0] = outs.tile([P, TILES * D], F32, name="tanh_c", tag="tanh_c")
                 tanh_of_cell_state(0, 0)
                 tanh_of_cell_state(0, 1)
                 cell_state(0, 3)
                 k_to_partitions(x_rows[2], x_grouped[2], 1, True)
-            if p >= 2:
-                hidden_state(p - 2, 3)
-            if p + 1 < CHUNKS:
-                h_grouped[p + 1] = new_grouped("h")
-                k_to_partitions(h_rows[p + 1], h_grouped[p + 1], 0, False)
-                k_to_partitions(h_rows[p + 1], h_grouped[p + 1], 1, True)
-                x_q[p + 1] = quantise(x_grouped[p + 1], mxops, "x")
+                h_grouped[2] = new_grouped("h")
+                k_to_partitions(h_rows[2], h_grouped[2], 0, False)
+                k_to_partitions(h_rows[2], h_grouped[2], 1, True)
+                x_q[2] = quantise(x_grouped[2], mxops, "x")
+
+                output[0] = gates.tile([P, FEATURE_TILES * CHUNK_ROWS], F32, name="output", tag="output")
+                half_gate(output[0], 0, w_o_q, u_o_q, 0, OUTPUT_BIAS)
+                tanh_of_cell_state(0, 2)
+                tanh_of_cell_state(0, 3)
+                h_q[2] = quantise(h_grouped[2], mxops, "h")
+                c_new[1] = outs.tile([P, TILES * D], F32, name="c_new", tag="c_new")
+                for t in range(3):
+                    cell_state(1, t)
+
+                half_gate(output[0], 1, w_o_q, u_o_q, 0, OUTPUT_BIAS)
+                tanh_c[1] = outs.tile([P, TILES * D], F32, name="tanh_c", tag="tanh_c")
+                tanh_of_cell_state(1, 0)
+                tanh_of_cell_state(1, 1)
+                cell_state(1, 3)
+                x_grouped[3] = new_grouped("x")
+                k_to_partitions(x_rows[3], x_grouped[3], 0, False)
+                k_to_partitions(x_rows[3], x_grouped[3], 1, False)
+                continue
+
+            if p < CHUNKS:
+                forget[p] = gates.tile([P, FEATURE_TILES * CHUNK_ROWS], F32, name="forget", tag="forget")
+                gate_tiles(forget[p], range(0, 3), w_f_q, u_f_q, p, FORGET_BIAS)
+            if p == CHUNKS:
+                output[p - 1] = gates.tile([P, FEATURE_TILES * CHUNK_ROWS], F32, name="output", tag="output")
+                gate_tiles(output[p - 1], range(0, 2), w_o_q, u_o_q, p - 1, OUTPUT_BIAS)
+            if p == 2:
+                tanh_of_cell_state(1, 2)
+                tanh_of_cell_state(1, 3)
+            if 2 < p <= CHUNKS:
+                tanh_c[p - 1] = outs.tile([P, TILES * D], F32, name="tanh_c", tag="tanh_c")
+                tanh_of_cell_state(p - 1, 0)
+                tanh_of_cell_state(p - 1, 1)
+            h_new[p - 2] = outs.tile([P, TILES * D], F32, name="h_new", tag="h_new")
+            for t in range(TILES):
+                hidden_state(p - 2, t)
+            if p == CHUNKS:
+                gate_tiles(output[p - 1], range(2, 4), w_o_q, u_o_q, p - 1, OUTPUT_BIAS)
+                tanh_of_cell_state(p - 1, 2)
+                tanh_of_cell_state(p - 1, 3)
             if p >= CHUNKS:
                 continue
 
+            gate_tiles(forget[p], range(3, 4), w_f_q, u_f_q, p, FORGET_BIAS)
             output[p - 1] = gates.tile([P, FEATURE_TILES * CHUNK_ROWS], F32, name="output", tag="output")
-            half_gate(output[p - 1], 0, w_o_q, u_o_q, p - 1, OUTPUT_BIAS)
-            if p == 1:
-                tanh_of_cell_state(0, 2)
-                tanh_of_cell_state(0, 3)
+            gate_tiles(output[p - 1], range(0, 2), w_o_q, u_o_q, p - 1, OUTPUT_BIAS)
             if p + 1 < CHUNKS:
-                h_q[p + 1] = quantise(h_grouped[p + 1], mxops, "h")
-            c_new[p] = outs.tile([P, TILES * D], F32, name="c_new", tag="c_new")
-            for t in range(3):
-                cell_state(p, t)
-
-            half_gate(output[p - 1], 1, w_o_q, u_o_q, p - 1, OUTPUT_BIAS)
-            tanh_c[p] = outs.tile([P, TILES * D], F32, name="tanh_c", tag="tanh_c")
-            tanh_of_cell_state(p, 0)
-            tanh_of_cell_state(p, 1)
-            cell_state(p, 3)
+                x_q[p + 1] = quantise(x_grouped[p + 1], mxops, "x")
+                h_grouped[p + 1] = new_grouped("h")
+                k_to_partitions(h_rows[p + 1], h_grouped[p + 1], 0, False)
+                k_to_partitions(h_rows[p + 1], h_grouped[p + 1], 1, True)
             if p + 2 < CHUNKS:
                 x_grouped[p + 2] = new_grouped("x")
                 k_to_partitions(x_rows[p + 2], x_grouped[p + 2], 0, False)
-                k_to_partitions(x_rows[p + 2], x_grouped[p + 2], 1, False)
+                k_to_partitions(x_rows[p + 2], x_grouped[p + 2], 1, True)
+            if p > 2:
+                tanh_of_cell_state(p - 1, 2)
+                tanh_of_cell_state(p - 1, 3)
+
+            gate_tiles(output[p - 1], range(2, 4), w_o_q, u_o_q, p - 1, OUTPUT_BIAS)
+            if p + 1 < CHUNKS:
+                h_q[p + 1] = quantise(h_grouped[p + 1], mxops, "h")
+            c_new[p] = outs.tile([P, TILES * D], F32, name="c_new", tag="c_new")
+            for t in range(TILES):
+                cell_state(p, t)

@@ -20,6 +20,7 @@ PSUM_BANKS = 8
 ROW_TILES = BATCH // P
 TILES = 4
 CHUNK_ROWS = TILES * P
+HALF_ROWS = CHUNK_ROWS // 2
 CHUNKS = ROW_TILES // TILES
 FEATURE_TILES = D // P
 STORE_TILES = 2
@@ -81,9 +82,9 @@ def tile_lstmcell_pb_t_kernel(
             nc.vector.quantize_mx(out=codes[:].bitcast(FP8X4), scales=scales[:], in_=grouped[:])
             return codes, scales
 
-        def prepare(rows, pool, tag):
+        def prepare(rows, pool, tag, first_on_scalar=False):
             grouped = new_grouped("first")
-            k_to_partitions(rows, grouped, 0, False)
+            k_to_partitions(rows, grouped, 0, first_on_scalar)
             k_to_partitions(rows, grouped, 1, True)
             return quantise(grouped, pool, tag)
 
@@ -109,6 +110,30 @@ def tile_lstmcell_pb_t_kernel(
                     in_=acc[:],
                     func=ACT.Sigmoid,
                     bias=gate_bias[:, first_bias + a : first_bias + a + 1],
+                    scale=1.0,
+                )
+
+        def output_of_rows(j, half):
+            rows = slice(half * HALF_ROWS, (half + 1) * HALF_ROWS)
+            for a in range(FEATURE_TILES):
+                features = slice(a * P, (a + 1) * P)
+                acc = banks.tile([P, HALF_ROWS], F32, name="bank", tag="bank")
+                for step, (weight, moving) in enumerate(((w_o_q, x_q[j]), (u_o_q, h_q[j]))):
+                    nc.tensor.matmul_mx(
+                        out=acc[:],
+                        lhsT=weight[0][:, features].bitcast(FP8X4),
+                        lhsT_scale=weight[1][:, features],
+                        rhs=moving[0][:, rows].bitcast(FP8X4),
+                        rhs_scale=moving[1][:, rows],
+                        start=(step == 0),
+                        stop=(step == 1),
+                    )
+                first = a * CHUNK_ROWS + half * HALF_ROWS
+                nc.scalar.activation(
+                    out=output[j][:, first : first + HALF_ROWS],
+                    in_=acc[:],
+                    func=ACT.Sigmoid,
+                    bias=gate_bias[:, OUTPUT_BIAS + a : OUTPUT_BIAS + a + 1],
                     scale=1.0,
                 )
 
@@ -190,10 +215,10 @@ def tile_lstmcell_pb_t_kernel(
 
         x_q, h_q = {}, {}
         forget, output, c_new, tanh_c, h_new, x_grouped, h_grouped = {}, {}, {}, {}, {}, {}, {}
-        w_f_q = prepare(w_f_rows, const, "W_f")
-        u_f_q = prepare(u_f_rows, const, "U_f")
-        x_q[0] = prepare(x_rows[0], mxops, "x")
-        h_q[0] = prepare(h_rows[0], mxops, "h")
+        w_f_q = prepare(w_f_rows, const, "W_f", False)
+        u_f_q = prepare(u_f_rows, const, "U_f", False)
+        x_q[0] = prepare(x_rows[0], mxops, "x", False)
+        h_q[0] = prepare(h_rows[0], mxops, "h", True)
 
         bias_bank = banks.tile([P, 2 * BANK], BF16, name="bank", tag="bank")
         nc.tensor.transpose(bias_bank[:, 0:P], bias_rows[:], ident_bf16[:])
@@ -277,7 +302,7 @@ def tile_lstmcell_pb_t_kernel(
                 gate_tiles(forget[p], range(0, 3), w_f_q, u_f_q, p, FORGET_BIAS)
             if p == CHUNKS:
                 output[p - 1] = gates.tile([P, FEATURE_TILES * CHUNK_ROWS], F32, name="output", tag="output")
-                gate_tiles(output[p - 1], range(0, 2), w_o_q, u_o_q, p - 1, OUTPUT_BIAS)
+                output_of_rows(p - 1, 0)
             if p == 2:
                 tanh_of_cell_state(1, 2)
                 tanh_of_cell_state(1, 3)
@@ -285,12 +310,13 @@ def tile_lstmcell_pb_t_kernel(
                 tanh_c[p - 1] = outs.tile([P, TILES * D], F32, name="tanh_c", tag="tanh_c")
                 tanh_of_cell_state(p - 1, 0)
                 tanh_of_cell_state(p - 1, 1)
+            if p == CHUNKS:
+                tanh_of_cell_state(p - 1, 2)
             h_new[p - 2] = outs.tile([P, TILES * D], F32, name="h_new", tag="h_new")
             for t in range(TILES):
                 hidden_state(p - 2, t)
             if p == CHUNKS:
-                gate_tiles(output[p - 1], range(2, 4), w_o_q, u_o_q, p - 1, OUTPUT_BIAS)
-                tanh_of_cell_state(p - 1, 2)
+                output_of_rows(p - 1, 1)
                 tanh_of_cell_state(p - 1, 3)
             if p >= CHUNKS:
                 continue
@@ -310,10 +336,15 @@ def tile_lstmcell_pb_t_kernel(
             if p > 2:
                 tanh_of_cell_state(p - 1, 2)
                 tanh_of_cell_state(p - 1, 3)
+            if p == CHUNKS - 1:
+                c_new[p] = outs.tile([P, TILES * D], F32, name="c_new", tag="c_new")
+                for t in range(TILES):
+                    cell_state(p, t)
 
             gate_tiles(output[p - 1], range(2, 4), w_o_q, u_o_q, p - 1, OUTPUT_BIAS)
             if p + 1 < CHUNKS:
                 h_q[p + 1] = quantise(h_grouped[p + 1], mxops, "h")
-            c_new[p] = outs.tile([P, TILES * D], F32, name="c_new", tag="c_new")
-            for t in range(TILES):
-                cell_state(p, t)
+            if p < CHUNKS - 1:
+                c_new[p] = outs.tile([P, TILES * D], F32, name="c_new", tag="c_new")
+                for t in range(TILES):
+                    cell_state(p, t)

@@ -189,6 +189,16 @@ def tile_lstmcell_pb_t_kernel(
         unused = const.tile([P, 1], F32, name="unused")
         nc.scalar.activation(out=unused[:], in_=zero[:], func=ACT.Sigmoid)
 
+        idle_rows = const.tile([P, D], BF16, name="idle_rows")
+        nc.vector.memset(idle_rows[:], 1.0)
+
+        def keep_warm(passes):
+            bank = banks.tile([P, BANK], F32, name="bank", tag="bank")
+            for i in range(passes):
+                nc.tensor.matmul(out=bank[:], lhsT=idle_rows[:, 0:P], rhs=idle_rows[:], start=True, stop=True)
+
+        keep_warm(4)
+
         x_view, h_view = by_row_tile(incoming), by_row_tile(h)
         c_view, cand_view = by_row_tile(c), by_row_tile(gated_cand)
         h_out, c_out = by_row_tile(out_0), by_row_tile(out_1)
@@ -216,9 +226,13 @@ def tile_lstmcell_pb_t_kernel(
         x_q, h_q = {}, {}
         forget, output, c_new, tanh_c, h_new, x_grouped, h_grouped = {}, {}, {}, {}, {}, {}, {}
         w_f_q = prepare(w_f_rows, const, "W_f", False)
+        keep_warm(1)
         u_f_q = prepare(u_f_rows, const, "U_f", False)
+        keep_warm(1)
         x_q[0] = prepare(x_rows[0], mxops, "x", False)
+        keep_warm(1)
         h_q[0] = prepare(h_rows[0], mxops, "h", True)
+        keep_warm(1)
 
         bias_bank = banks.tile([P, 2 * BANK], BF16, name="bank", tag="bank")
         nc.tensor.transpose(bias_bank[:, 0:P], bias_rows[:], ident_bf16[:])

@@ -26,6 +26,7 @@ FEATURE_TILES = D // P
 STORE_TILES = 2
 LOADS_AHEAD = 3
 
+SHIFT = 128
 FLOPS = 4 * 2 * BATCH * D * D
 
 
@@ -77,9 +78,12 @@ def tile_lstmcell_pb_t_kernel(
                 nc.vector.tensor_copy(out=grouped_words[:, 2 * pair : 2 * pair + 2, :, :], in_=side_by_side)
 
         def quantise(grouped, pool, tag):
-            codes = pool.tile([P, TILES * P], U32, name="codes_" + tag, tag="codes_" + tag, align_bytes=64)
-            scales = pool.tile([P, TILES * P], U8, name="scales_" + tag, tag="scales_" + tag, align_bytes=64)
-            nc.vector.quantize_mx(out=codes[:].bitcast(FP8X4), scales=scales[:], in_=grouped[:])
+            shift = SHIFT if pool is const else 0
+            codes = pool.tile([P, TILES * P + shift // 4], U32, name="codes_" + tag, tag="codes_" + tag, align_bytes=256)
+            scales = pool.tile([P, TILES * P + shift], U8, name="scales_" + tag, tag="scales_" + tag, align_bytes=256)
+            codes = codes[:, shift // 4 : shift // 4 + TILES * P]
+            scales = scales[:, shift : shift + TILES * P]
+            nc.vector.quantize_mx(out=codes.bitcast(FP8X4), scales=scales, in_=grouped[:])
             return codes, scales
 
         def prepare(rows, pool, tag, first_on_scalar=False):
@@ -100,8 +104,8 @@ def tile_lstmcell_pb_t_kernel(
                         out=acc[:],
                         lhsT=weight[0][:, features].bitcast(FP8X4),
                         lhsT_scale=weight[1][:, features],
-                        rhs=moving[0][:].bitcast(FP8X4),
-                        rhs_scale=moving[1][:],
+                        rhs=moving[0].bitcast(FP8X4),
+                        rhs_scale=moving[1],
                         start=(step == 0),
                         stop=(step == 1),
                     )

from contextlib import ExitStack

import concourse.mybir as mybir
from concourse.masks import make_identity

F32 = mybir.dt.float32
BF16 = mybir.dt.bfloat16
U32 = mybir.dt.uint32
U8 = mybir.dt.uint8
FP8X4 = mybir.dt.float8_e4m3fn_x4
ACT = mybir.ActivationFunctionType
ALU = mybir.AluOpType

P = 128
PACK = 4
BATCH = 4096
D = 512
BANK = 512
PSUM_BANKS = 8
ROW_TILES = BATCH // P
TILES = 4
CHUNK_ROWS = TILES * P
HALF_ROWS = CHUNK_ROWS // 2
CHUNKS = ROW_TILES // TILES
FEATURE_TILES = D // P
STORE_TILES = 2
LOADS_AHEAD = 3

SHIFT = 128
FLOPS = 4 * 2 * BATCH * D * D


def tile_lstmcell_pb_t_kernel(
    tc, incoming, h, c, gated_cand, W_f, b_W_f, W_o, b_W_o, U_f, b_U_f, U_o, b_U_o, out_0, out_1
):
    nc = tc.nc

    def by_row_tile(ap):
        return ap.rearrange("(p t) d -> p t d", t=ROW_TILES)

    def by_feature_tile(ap):
        return ap.rearrange("(a p) k -> p a k", p=P)

    with ExitStack() as ctx:
        const = ctx.enter_context(tc.tile_pool(name="const", bufs=1))
        acts = ctx.enter_context(tc.tile_pool(name="acts", bufs=LOADS_AHEAD))
        state = ctx.enter_context(tc.tile_pool(name="state", bufs=LOADS_AHEAD + 1))
        stage = ctx.enter_context(tc.tile_pool(name="stage", bufs=2))
        mxops = ctx.enter_context(tc.tile_pool(name="mxops", bufs=3))
        gates = ctx.enter_context(tc.tile_pool(name="gates", bufs=2))
        outs = ctx.enter_context(tc.tile_pool(name="outs", bufs=3))
        banks = ctx.enter_context(tc.psum_pool(name="banks", bufs=PSUM_BANKS))
        ctx.enter_context(tc.manual_schedule())

        def load(view, first_tile, pool, tag):
            rows = pool.tile([P, TILES * D], BF16, name=tag, tag=tag)
            nc.sync.dma_start(
                out=rows[:].rearrange("p (t d) -> p t d", t=TILES),
                in_=view[:, first_tile : first_tile + TILES, :],
            )
            return rows

        def new_grouped(tag):
            return stage.tile([P, TILES * P * PACK], BF16, name="grouped_" + tag, tag="grouped_" + tag, align_bytes=64)

        def k_to_partitions(rows, grouped, pair, on_scalar):
            row_words = rows[:].bitcast(F32).rearrange("r (t u q) -> r t u q", t=TILES, u=2)
            grouped_words = grouped[:].bitcast(F32).rearrange("q (t r u) -> q t r u", t=TILES, u=2)
            bank = banks.tile([P, BANK], F32, name="bank", tag="bank")
            turned = bank[:].rearrange("q (i u r) -> q i u r", i=2, u=2)
            for i in range(2):
                for u in range(2):
                    nc.tensor.transpose(turned[:, i, u, :], row_words[:, 2 * pair + i, u, :], ident[:])
            side_by_side = turned.rearrange("q i u r -> q i r u")
            if on_scalar:
                nc.scalar.copy(out=grouped_words[:, 2 * pair : 2 * pair + 2, :, :], in_=side_by_side)
            else:
                nc.vector.tensor_copy(out=grouped_words[:, 2 * pair : 2 * pair + 2, :, :], in_=side_by_side)

        def quantise(grouped, pool, tag):
            shift = SHIFT if pool is const else 0
            codes = pool.tile([P, TILES * P + shift // 4], U32, name="codes_" + tag, tag="codes_" + tag, align_bytes=256)
            scales = pool.tile([P, TILES * P + shift], U8, name="scales_" + tag, tag="scales_" + tag, align_bytes=256)
            codes = codes[:, shift // 4 : shift // 4 + TILES * P]
            scales = scales[:, shift : shift + TILES * P]
            nc.vector.quantize_mx(out=codes.bitcast(FP8X4), scales=scales, in_=grouped[:])
            return codes, scales

        def prepare(rows, pool, tag, first_on_scalar=False):
            grouped = new_grouped("first")
            k_to_partitions(rows, grouped, 0, first_on_scalar)
            k_to_partitions(rows, grouped, 1, True)
            return quantise(grouped, pool, tag)

        def half_gate(gate, half, w_in, w_rec, j, first_bias):
            gate_tiles(gate, range(2 * half, 2 * half + 2), w_in, w_rec, j, first_bias)

        def gate_tiles(gate, tiles, w_in, w_rec, j, first_bias):
            for a in tiles:
                features = slice(a * P, (a + 1) * P)
                acc = banks.tile([P, BANK], F32, name="bank", tag="bank")
                for step, (weight, moving) in enumerate(((w_in, x_q[j]), (w_rec, h_q[j]))):
                    nc.tensor.matmul_mx(
                        out=acc[:],
                        lhsT=weight[0][:, features].bitcast(FP8X4),
                        lhsT_scale=weight[1][:, features],
                        rhs=moving[0].bitcast(FP8X4),
                        rhs_scale=moving[1],
                        start=(step == 0),
                        stop=(step == 1),
                    )
                nc.scalar.activation(
                    out=gate[:, a * CHUNK_ROWS : (a + 1) * CHUNK_ROWS],
                    in_=acc[:],
                    func=ACT.Sigmoid,
                    bias=gate_bias[:, first_bias + a : first_bias + a + 1],
                    scale=1.0,
                )

        def output_of_rows(j, half):
            rows = slice(half * HALF_ROWS, (half + 1) * HALF_ROWS)
            for a in range(FEATURE_TILES):
                features = slice(a * P, (a + 1) * P)
                acc = banks.tile([P, HALF_ROWS], F32, name="bank", tag="bank")
                for step, (weight, moving) in enumerate(((w_o_q, x_q[j]), (u_o_q, h_q[j]))):
                    nc.tensor.matmul_mx(
                        out=acc[:],
                        lhsT=weight[0][:, features].bitcast(FP8X4),
                        lhsT_scale=weight[1][:, features],
                        rhs=moving[0][:, rows].bitcast(FP8X4),
                        rhs_scale=moving[1][:, rows],
                        start=(step == 0),
                        stop=(step == 1),
                    )
                first = a * CHUNK_ROWS + half * HALF_ROWS
                nc.scalar.activation(
                    out=output[j][:, first : first + HALF_ROWS],
                    in_=acc[:],
                    func=ACT.Sigmoid,
                    bias=gate_bias[:, OUTPUT_BIAS + a : OUTPUT_BIAS + a + 1],
                    scale=1.0,
                )

        def gate_by_row(gate, t):
            bank = banks.tile([P, BANK], F32, name="bank", tag="bank")
            for a in range(FEATURE_TILES):
                first = a * CHUNK_ROWS + t * P
                nc.tensor.transpose(bank[:, a * P : (a + 1) * P], gate[:, first : first + P], ident[:])
            return bank

        def store(view, j, t, result, alone=False):
            if alone:
                nc.sync.dma_start(out=view[:, j * TILES + t, :], in_=result[:, t * D : (t + 1) * D])
            elif (t + 1) % STORE_TILES == 0:
                first = t + 1 - STORE_TILES
                nc.sync.dma_start(
                    out=view[:, j * TILES + first : j * TILES + t + 1, :],
                    in_=result[:, first * D : (t + 1) * D].rearrange("p (t d) -> p t d", t=STORE_TILES),
                )

        def cell_state(j, t):
            cols = slice(t * D, (t + 1) * D)
            forget_rows = gate_by_row(forget[j], t)
            nc.vector.tensor_tensor(out=c_new[j][:, cols], in0=forget_rows[:], in1=c_rows[j][:, cols], op=ALU.mult)
            nc.gpsimd.tensor_tensor(out=c_new[j][:, cols], in0=c_new[j][:, cols], in1=cand_rows[j][:, cols], op=ALU.add)
            store(c_out, j, t, c_new[j], alone=(j == CHUNKS - 1))

        def tanh_of_cell_state(j, t):
            cols = slice(t * D, (t + 1) * D)
            nc.scalar.activation(out=tanh_c[j][:, cols], in_=c_new[j][:, cols], func=ACT.Tanh)

        def hidden_state(j, t):
            cols = slice(t * D, (t + 1) * D)
            output_rows = gate_by_row(output[j], t)
            nc.vector.tensor_tensor(out=h_new[j][:, cols], in0=output_rows[:], in1=tanh_c[j][:, cols], op=ALU.mult)
            store(h_out, j, t, h_new[j], alone=(j == CHUNKS - 1))

        bias_rows = const.tile([P, P], BF16, name="bias_rows")
        nc.gpsimd.memset(bias_rows[:], 0.0)
        for v, vector in enumerate((b_W_f, b_W_o, b_U_f, b_U_o)):
            nc.scalar.dma_start(
                out=bias_rows[v * FEATURE_TILES : (v + 1) * FEATURE_TILES, :],
                in_=vector.rearrange("(a p) -> a p", p=P),
            )

        ident = const.tile([P, P], F32, name="ident")
        make_identity(nc, ident[:])
        ident_bf16 = const.tile([P, P], BF16, name="ident_bf16")
        make_identity(nc, ident_bf16[:])

        zero = const.tile([P, 1], F32, name="zero")
        nc.vector.memset(zero[:], 0.0)
        unused = const.tile([P, 1], F32, name="unused")
        nc.scalar.activation(out=unused[:], in_=zero[:], func=ACT.Sigmoid)

        idle_rows = const.tile([P, D], BF16, name="idle_rows")
        nc.vector.memset(idle_rows[:], 1.0)

        def keep_warm(passes):
            bank = banks.tile([P, BANK], F32, name="bank", tag="bank")
            for i in range(passes):
                nc.tensor.matmul(out=bank[:], lhsT=idle_rows[:, 0:P], rhs=idle_rows[:], start=True, stop=True)

        keep_warm(4)

        x_view, h_view = by_row_tile(incoming), by_row_tile(h)
        c_view, cand_view = by_row_tile(c), by_row_tile(gated_cand)
        h_out, c_out = by_row_tile(out_0), by_row_tile(out_1)
        x_rows, h_rows, c_rows, cand_rows = {}, {}, {}, {}

        def load_acts(j):
            x_rows[j] = load(x_view, j * TILES, acts, "x")
            h_rows[j] = load(h_view, j * TILES, acts, "h")

        def load_state(j):
            c_rows[j] = load(c_view, j * TILES, state, "c")
            cand_rows[j] = load(cand_view, j * TILES, state, "cand")

        w_f_rows = load(by_feature_tile(W_f), 0, const, "W_f")
        u_f_rows = load(by_feature_tile(U_f), 0, const, "U_f")
        load_acts(0)
        load_acts(1)
        w_o_rows = load(by_feature_tile(W_o), 0, const, "W_o")
        u_o_rows = load(by_feature_tile(U_o), 0, const, "U_o")
        load_state(0)
        load_acts(2)
        load_state(1)
        load_state(2)

        x_q, h_q = {}, {}
        forget, output, c_new, tanh_c, h_new, x_grouped, h_grouped = {}, {}, {}, {}, {}, {}, {}
        w_f_q = prepare(w_f_rows, const, "W_f", False)
        keep_warm(1)
        u_f_q = prepare(u_f_rows, const, "U_f", False)
        keep_warm(1)
        x_q[0] = prepare(x_rows[0], mxops, "x", False)
        keep_warm(1)
        h_q[0] = prepare(h_rows[0], mxops, "h", True)
        keep_warm(1)

        bias_bank = banks.tile([P, 2 * BANK], BF16, name="bank", tag="bank")
        nc.tensor.transpose(bias_bank[:, 0:P], bias_rows[:], ident_bf16[:])
        bias_columns = const.tile([P, 4 * FEATURE_TILES], F32, name="bias_columns")
        nc.vector.tensor_copy(out=bias_columns[:], in_=bias_bank[:, 0 : 4 * FEATURE_TILES])
        gate_bias = const.tile([P, 2 * FEATURE_TILES], F32, name="gate_bias")
        nc.vector.tensor_tensor(
            out=gate_bias[:],
            in0=bias_columns[:, 0 : 2 * FEATURE_TILES],
            in1=bias_columns[:, 2 * FEATURE_TILES : 4 * FEATURE_TILES],
            op=ALU.add,
        )
        FORGET_BIAS, OUTPUT_BIAS = 0, FEATURE_TILES
        x_grouped[1] = new_grouped("x")
        k_to_partitions(x_rows[1], x_grouped[1], 0, False)
        k_to_partitions(x_rows[1], x_grouped[1], 1, True)

        for p in range(CHUNKS + 2):
            if p == 1:
                load_acts(3)
            if 0 < p and p + LOADS_AHEAD < CHUNKS:
                load_acts(p + LOADS_AHEAD)
            if 0 < p and p + LOADS_AHEAD - 1 < CHUNKS:
                load_state(p + LOADS_AHEAD - 1)

            if p < 2:
                forget[p] = gates.tile([P, FEATURE_TILES * CHUNK_ROWS], F32, name="forget", tag="forget")
                half_gate(forget[p], 0, w_f_q, u_f_q, p, FORGET_BIAS)
                if p == 0:
                    h_grouped[1] = new_grouped("h")
                    k_to_partitions(h_rows[1], h_grouped[1], 0, False)
                    k_to_partitions(h_rows[1], h_grouped[1], 1, True)
                    x_q[1] = quantise(x_grouped[1], mxops, "x")
                    w_o_grouped = new_grouped("first")
                    k_to_partitions(w_o_rows, w_o_grouped, 0, False)
                if p == 1:
                    c_new[0] = outs.tile([P, TILES * D], F32, name="c_new", tag="c_new")
                    for t in range(3):
                        cell_state(0, t)
                    x_grouped[2] = new_grouped("x")
                    k_to_partitions(x_rows[2], x_grouped[2], 0, True)

                half_gate(forget[p], 1, w_f_q, u_f_q, p, FORGET_BIAS)
                if p == 0:
                    k_to_partitions(w_o_rows, w_o_grouped, 1, True)
                    h_q[1] = quantise(h_grouped[1], mxops, "h")
                    w_o_q = quantise(w_o_grouped, const, "W_o")
                    u_o_q = prepare(u_o_rows, const, "U_o")
                    continue
                tanh_c[0] = outs.tile([P, TILES * D], F32, name="tanh_c", tag="tanh_c")
                tanh_of_cell_state(0, 0)
                tanh_of_cell_state(0, 1)
                cell_state(0, 3)
                k_to_partitions(x_rows[2], x_grouped[2], 1, True)
                h_grouped[2] = new_grouped("h")
                k_to_partitions(h_rows[2], h_grouped[2], 0, False)
                k_to_partitions(h_rows[2], h_grouped[2], 1, True)
                x_q[2] = quantise(x_grouped[2], mxops, "x")

                output[0] = gates.tile([P, FEATURE_TILES * CHUNK_ROWS], F32, name="output", tag="output")
                half_gate(output[0], 0, w_o_q, u_o_q, 0, OUTPUT_BIAS)
                tanh_of_cell_state(0, 2)
                tanh_of_cell_state(0, 3)
                h_q[2] = quantise(h_grouped[2], mxops, "h")
                c_new[1] = outs.tile([P, TILES * D], F32, name="c_new", tag="c_new")
                for t in range(3):
                    cell_state(1, t)

                half_gate(output[0], 1, w_o_q, u_o_q, 0, OUTPUT_BIAS)
                tanh_c[1] = outs.tile([P, TILES * D], F32, name="tanh_c", tag="tanh_c")
                tanh_of_cell_state(1, 0)
                tanh_of_cell_state(1, 1)
                cell_state(1, 3)
                x_grouped[3] = new_grouped("x")
                k_to_partitions(x_rows[3], x_grouped[3], 0, False)
                k_to_partitions(x_rows[3], x_grouped[3], 1, False)
                continue

            if p < CHUNKS:
                forget[p] = gates.tile([P, FEATURE_TILES * CHUNK_ROWS], F32, name="forget", tag="forget")
                gate_tiles(forget[p], range(0, 3), w_f_q, u_f_q, p, FORGET_BIAS)
            if p == CHUNKS:
                output[p - 1] = gates.tile([P, FEATURE_TILES * CHUNK_ROWS], F32, name="output", tag="output")
                output_of_rows(p - 1, 0)
            if p == 2:
                tanh_of_cell_state(1, 2)
                tanh_of_cell_state(1, 3)
            if 2 < p <= CHUNKS:
                tanh_c[p - 1] = outs.tile([P, TILES * D], F32, name="tanh_c", tag="tanh_c")
                tanh_of_cell_state(p - 1, 0)
                tanh_of_cell_state(p - 1, 1)
            if p == CHUNKS:
                tanh_of_cell_state(p - 1, 2)
            h_new[p - 2] = outs.tile([P, TILES * D], F32, name="h_new", tag="h_new")
            for t in range(TILES):
                hidden_state(p - 2, t)
            if p == CHUNKS:
                output_of_rows(p - 1, 1)
                tanh_of_cell_state(p - 1, 3)
            if p >= CHUNKS:
                continue

            gate_tiles(forget[p], range(3, 4), w_f_q, u_f_q, p, FORGET_BIAS)
            output[p - 1] = gates.tile([P, FEATURE_TILES * CHUNK_ROWS], F32, name="output", tag="output")
            gate_tiles(output[p - 1], range(0, 2), w_o_q, u_o_q, p - 1, OUTPUT_BIAS)
            if p + 1 < CHUNKS:
                x_q[p + 1] = quantise(x_grouped[p + 1], mxops, "x")
                h_grouped[p + 1] = new_grouped("h")
                k_to_partitions(h_rows[p + 1], h_grouped[p + 1], 0, False)
                k_to_partitions(h_rows[p + 1], h_grouped[p + 1], 1, True)
            if p + 2 < CHUNKS:
                x_grouped[p + 2] = new_grouped("x")
                k_to_partitions(x_rows[p + 2], x_grouped[p + 2], 0, False)
                k_to_partitions(x_rows[p + 2], x_grouped[p + 2], 1, True)
            if p > 2:
                tanh_of_cell_state(p - 1, 2)
                tanh_of_cell_state(p - 1, 3)
            if p == CHUNKS - 1:
                c_new[p] = outs.tile([P, TILES * D], F32, name="c_new", tag="c_new")
                for t in range(TILES):
                    cell_state(p, t)

            gate_tiles(output[p - 1], range(2, 4), w_o_q, u_o_q, p - 1, OUTPUT_BIAS)
            if p + 1 < CHUNKS:
                h_q[p + 1] = quantise(h_grouped[p + 1], mxops, "h")
            if p < CHUNKS - 1:
                c_new[p] = outs.tile([P, TILES * D], F32, name="c_new", tag="c_new")
                for t in range(TILES):
                    cell_state(p, t)
